import numpy as np
import ml_dtypes


def mxq(x, axis, fmt="e4m3"):
    dtype, down = {"e4m3": (ml_dtypes.float8_e4m3fn, 7), "e5m2": (ml_dtypes.float8_e5m2, 14)}[fmt]
    v = np.moveaxis(np.asarray(x, np.float32).astype(ml_dtypes.bfloat16).astype(np.float64), axis, -1)
    blocks = v.reshape(v.shape[:-1] + (-1, 32))
    amax = np.abs(blocks).max(-1, keepdims=True)
    byte = np.maximum(np.where(amax > 0, np.frexp(amax)[1] - 1 + 127, 0) - down, 1)
    scale = np.exp2(byte - 127.0)
    codes = (blocks / scale).astype(np.float32).astype(dtype).astype(np.float64)
    return np.moveaxis((codes * scale).reshape(v.shape), -1, axis)


WIDE = False


def mx_kscale(k):
    if not WIDE:
        return np.ones(k)
    levels = np.array([10, -10, 5, -5, 0])
    a = np.random.permutation(np.resize(levels, k // 512 * 4)).reshape(k // 512, 4)
    idx = np.arange(k)
    return np.exp2(a[idx // 512, idx % 128 // 32])


BF16 = ml_dtypes.bfloat16


def bf(x):
    return np.asarray(x, np.float32).astype(BF16)


def f64(x):
    return np.asarray(x).astype(np.float64)


E2M1 = np.array([0.0, 0.5, 1.0, 1.5, 2.0, 3.0, 4.0, 6.0, -0.0, -0.5, -1.0, -1.5, -2.0, -3.0, -4.0, -6.0])


def pack_weight(w, fmt):
    k, n = w.shape
    w = f64(bf(w)).reshape(k // 32, 32, n)
    amax = np.abs(w).max(1)
    if fmt == "e4m3":
        byte = np.frexp(amax)[1] - 1 + 127 - 7
    else:
        mant, ex = np.frexp(amax / 6.0)
        byte = np.where(mant > 0.5, ex, ex - 1) + 127
    byte = np.clip(np.where(amax > 0, byte, 1), 1, 254)
    scaled = (w * np.exp2(127.0 - byte)[:, None, :]).reshape(k, n).astype(np.float32)
    by_word = np.ascontiguousarray(scaled.reshape(k // 512, 128, 4, n).transpose(0, 1, 3, 2))
    if fmt == "e4m3":
        words = by_word.astype(ml_dtypes.float8_e4m3fn).view(np.uint8)
    else:
        c = by_word.astype(ml_dtypes.float4_e2m1fn).view(np.uint8) & 0xF
        words = c[..., 0::2] | (c[..., 1::2] << 4)
    return np.ascontiguousarray(words), np.ascontiguousarray(byte.astype(np.uint8).reshape(k // 512, 16, n))


def unpack_weight(words, scales, fmt):
    g, p, n, _ = words.shape
    if fmt == "e4m3":
        vals = np.ascontiguousarray(words).view(ml_dtypes.float8_e4m3fn).astype(np.float64)
    else:
        nib = np.empty((g, p, n, 4), np.uint8)
        nib[..., 0::2] = words & 0xF
        nib[..., 1::2] = words >> 4
        vals = E2M1[nib]
    vals = vals * np.repeat(np.exp2(scales.astype(np.float64) - 127.0), 8, axis=1)[..., None]
    return vals.transpose(0, 1, 3, 2).reshape(g * 512, n)


B, S, E, H, D, XL, TOPK = 8, 1024, 1024, 2, 64, 512, 8
HD = H * D
FMT = "e4m3"


def l2norm(x):
    return x / np.maximum(np.sqrt((x * x).sum(-1, keepdims=True)), 1e-12)


def split_heads(x):
    return x.reshape(B, S, H, D).transpose(0, 2, 1, 3)


def setup_inputs():
    n = np.random.standard_normal
    s = mx_kscale(E)
    x = bf(n((B, S, E)) * s)
    Wq_words, Wq_scales = pack_weight((n((HD, E)) / np.sqrt(E) / s).T, FMT)
    bq = bf(n(HD) * 0.1)
    Wk_words, Wk_scales = pack_weight((n((HD, E)) / np.sqrt(E) / s).T, FMT)
    bk = bf(n(HD) * 0.1)
    Wv_words, Wv_scales = pack_weight((n((HD, E)) / np.sqrt(E) / s).T, FMT)
    bv = bf(n(HD) * 0.1)
    return {"input": x,
            "Wq_words": Wq_words, "Wq_scales": Wq_scales, "bq": bq,
            "Wk_words": Wk_words, "Wk_scales": Wk_scales, "bk": bk,
            "Wv_words": Wv_words, "Wv_scales": Wv_scales, "bv": bv}


def reference(input, Wq_words, Wq_scales, bq, Wk_words, Wk_scales, bk, Wv_words, Wv_scales, bv):
    xq = mxq(f64(input), 2, "e4m3")
    q = split_heads(l2norm((xq @ unpack_weight(Wq_words, Wq_scales, FMT)) + f64(bq)))
    k = split_heads(l2norm((xq @ unpack_weight(Wk_words, Wk_scales, FMT)) + f64(bk)))
    v = split_heads((xq @ unpack_weight(Wv_words, Wv_scales, FMT)) + f64(bv))
    return q, k, v

@@ -1,0 +1,222 @@
+from contextlib import ExitStack
+
+import concourse.mybir as mybir
+from concourse.masks import make_identity
+
+F32 = mybir.dt.float32
+BF16 = mybir.dt.bfloat16
+I32 = mybir.dt.int32
+U32 = mybir.dt.uint32
+U8 = mybir.dt.uint8
+FP8X4 = mybir.dt.float8_e4m3fn_x4
+ALU = mybir.AluOpType
+ACT = mybir.ActivationFunctionType
+
+P = 128
+PACK = 4
+K_PASS = P * PACK
+BATCH, SEQ, EMB = 8, 1024, 1024
+HEADS, HEAD_DIM = 2, 64
+FEAT = HEADS * HEAD_DIM
+PROJ = 3
+PASSES = EMB // K_PASS
+WORDS = K_PASS // 2
+TOK_PER_PART = SEQ // P
+TILES = 4
+ROUNDS = BATCH * TOK_PER_PART // TILES
+ROUNDS_PER_BATCH = TOK_PER_PART // TILES
+X_BUFS = 8
+
+FLOPS = 2 * BATCH * SEQ * EMB * PROJ * FEAT
+
+
+def tile_knnxlmultiheadsattention_pa_t_kernel(
+    tc, x, wq_words, wq_scales, bq, wk_words, wk_scales, bk, wv_words, wv_scales, bv, out_q, out_k, out_v
+):
+    nc = tc.nc
+    weights = ((wq_words, wq_scales, bq), (wk_words, wk_scales, bk), (wv_words, wv_scales, bv))
+    outs = (out_q, out_k, out_v)
+    x_view = x.rearrange("b (p j) k -> b p j k", j=TOK_PER_PART)
+
+    with ExitStack() as ctx:
+        ctx.enter_context(tc.manual_schedule())
+        const = ctx.enter_context(tc.tile_pool(name="const", bufs=1))
+        x_pool = ctx.enter_context(tc.tile_pool(name="x", bufs=X_BUFS))
+        grouped_pool = ctx.enter_context(tc.tile_pool(name="grouped", bufs=2))
+        mx_pool = ctx.enter_context(tc.tile_pool(name="mx", bufs=2))
+        stage_pool = ctx.enter_context(tc.tile_pool(name="stage", bufs=3))
+        small_pool = ctx.enter_context(tc.tile_pool(name="small", bufs=3))
+        xt_pool = ctx.enter_context(tc.psum_pool(name="xt", bufs=TILES))
+        acc_pool = ctx.enter_context(tc.psum_pool(name="acc", bufs=TILES))
+
+        x_tiles = {}
+        grouped_tiles = {}
+        code_tiles = {}
+        plane_tiles = {}
+        acc_tiles = {}
+        stage_tiles = {}
+        norm_tiles = {}
+        inv_tiles = {}
+
+        def load(r):
+            b, half = divmod(r, ROUNDS_PER_BATCH)
+            x_sb = x_pool.tile([P, TILES, EMB], BF16)
+            nc.sync.dma_start(out=x_sb[:], in_=x_view[b, :, half * TILES : (half + 1) * TILES, :])
+            x_tiles[r] = x_sb
+
+        def transpose(r):
+            x_words = x_tiles[r][:].rearrange("p i k -> p (i k)").bitcast(F32)
+            grouped = grouped_pool.tile([P, TILES, PASSES, P, PACK], BF16, align_bytes=64)
+            grouped_words = (
+                grouped[:]
+                .rearrange("p i g w t -> p (i g w t)")
+                .bitcast(F32)
+                .rearrange("p (i g w u) -> p i g w u", i=TILES, g=PASSES, u=2)
+            )
+            for i in range(TILES):
+                xt = xt_pool.tile([P, PASSES, 2, P], F32)
+                for g in range(PASSES):
+                    first = (i * PASSES + g) * WORDS
+                    for u in range(2):
+                        nc.tensor.transpose(xt[:, g, u, :], x_words[:, first + u : first + WORDS : 2], ident[:])
+                planes_in_turn = xt[:].rearrange("p g u w -> p g w u")
+                if i < TILES - 1:
+                    nc.scalar.copy(out=grouped_words[:, i], in_=planes_in_turn)
+                else:
+                    nc.vector.tensor_copy(out=grouped_words[:, i], in_=planes_in_turn)
+            grouped_tiles[r] = grouped
+            if r + X_BUFS < ROUNDS:
+                load(r + X_BUFS)
+
+        def quantise(r):
+            codes = mx_pool.tile([P, TILES * PASSES * P], U32, align_bytes=64)
+            planes = mx_pool.tile([P, TILES * PASSES * P], U8, align_bytes=64)
+            nc.vector.quantize_mx(
+                out=codes[:].bitcast(FP8X4),
+                scales=planes[:],
+                in_=grouped_tiles[r][:].rearrange("p i g w t -> p (i g w t)"),
+            )
+            code_tiles[r] = codes
+            plane_tiles[r] = planes
+
+        def project(r):
+            codes = code_tiles[r]
+            planes = plane_tiles[r]
+            for i in range(TILES):
+                acc = acc_pool.tile([P, 512], F32)
+                for cols in (slice(0, 2 * FEAT), slice(2 * FEAT, 3 * FEAT)):
+                    for g in range(PASSES):
+                        tokens = slice((i * PASSES + g) * P, (i * PASSES + g + 1) * P)
+                        nc.tensor.matmul_mx(
+                            out=acc[:, cols],
+                            lhsT=codes[:, tokens].bitcast(FP8X4),
+                            lhsT_scale=planes[:, tokens],
+                            rhs=w_codes[:, g, cols].bitcast(FP8X4),
+                            rhs_scale=w_planes[:, g, cols],
+                            start=(g == 0),
+                            stop=(g == PASSES - 1),
+                        )
+                acc_tiles[(r, i)] = acc
+
+        def add_bias(r):
+            b, half = divmod(r, ROUNDS_PER_BATCH)
+            if half == 0:
+                stage = stage_pool.tile([P, PROJ, HEADS, TOK_PER_PART, HEAD_DIM], F32)
+                stage_tiles[b] = stage
+            stage = stage_tiles[b]
+            for i in range(TILES):
+                nc.vector.tensor_tensor(
+                    out=stage[:, :, :, half * TILES + i, :],
+                    in0=acc_tiles[(r, i)][:, 0 : PROJ * FEAT].rearrange("p (w h d) -> p w h d", w=PROJ, h=HEADS),
+                    in1=bias_bc[:].rearrange("p (w h d) -> p w h d", w=PROJ, h=HEADS),
+                    op=ALU.add,
+                )
+
+        def sum_squares(r):
+            b, half = divmod(r, ROUNDS_PER_BATCH)
+            stage = stage_tiles[b]
+            squares = small_pool.tile([P, 2, TILES, HEADS, HEAD_DIM], BF16)
+            sumsq = small_pool.tile([P, 2, TILES], F32)
+            for i in range(TILES):
+                for w in range(2):
+                    nc.scalar.activation(
+                        out=squares[:, w, i],
+                        in_=stage[:, w, :, half * TILES + i, :],
+                        func=ACT.Square,
+                        accum_out=sumsq[:, w, i : i + 1],
+                    )
+            norm = small_pool.tile([P, 2, TILES], F32)
+            nc.scalar.sqrt(norm[:], sumsq[:])
+            norm_tiles[r] = norm
+
+        def inverse_norms(r):
+            floored = small_pool.tile([P, 2, TILES], F32)
+            inv = small_pool.tile([P, 2, TILES], F32)
+            nc.vector.tensor_scalar_max(floored[:], norm_tiles[r][:], 1e-12)
+            nc.vector.reciprocal(inv[:], floored[:])
+            inv_tiles[r] = inv
+
+        def scale(r):
+            b, half = divmod(r, ROUNDS_PER_BATCH)
+            stage = stage_tiles[b]
+            for w in range(2):
+                part = stage[:, w, :, half * TILES : (half + 1) * TILES, :]
+                nc.gpsimd.tensor_tensor(
+                    out=part,
+                    in0=part,
+                    in1=inv_tiles[r][:, w, :].unsqueeze(1).unsqueeze(3).to_broadcast([P, HEADS, TILES, HEAD_DIM]),
+                    op=ALU.mult,
+                )
+
+        def store(b, w):
+            nc.sync.dma_start(
+                out=outs[w][b].rearrange("h (p j) d -> p h (j d)", j=TOK_PER_PART),
+                in_=stage_tiles[b][:, w].rearrange("p h j d -> p h (j d)"),
+            )
+
+        ident = const.tile([P, P], F32)
+        make_identity(nc, ident[:])
+        w_codes = const.tile([P, PASSES, PROJ * FEAT], U32, align_bytes=64)
+        w_planes = const.tile([P, PASSES, PROJ * FEAT], U8, align_bytes=64)
+        bias_bc = const.tile([P, PROJ * FEAT], BF16)
+        nc.vector.memset(w_planes[:].rearrange("p g n -> p (g n)").bitcast(I32), 0)
+        warm = const.tile([P, 1], F32)
+        nc.vector.memset(warm[:], 1.0)
+        nc.scalar.sqrt(warm[:], warm[:])
+
+        for w, (words, scales, bias) in enumerate(weights):
+            cols = slice(w * FEAT, (w + 1) * FEAT)
+            nc.sync.dma_start(
+                out=w_codes[:, :, cols].bitcast(I32), in_=words.rearrange("g p n t -> p g (n t)").bitcast(I32)
+            )
+            rows = scales.bitcast(I32).rearrange("g (q r) n -> r q g n", r=4)
+            for r in range(4):
+                nc.sync.dma_start(out=w_planes[r:P:32, :, cols].bitcast(I32), in_=rows[r])
+        load(0)
+        load(1)
+        for w, (words, scales, bias) in enumerate(weights):
+            nc.sync.dma_start(out=bias_bc[:, w * FEAT : (w + 1) * FEAT], in_=bias.partition_broadcast(P))
+        for r in range(2, X_BUFS):
+            load(r)
+
+        transpose(0)
+        quantise(0)
+        for t in range(ROUNDS + 1):
+            if t + 1 < ROUNDS:
+                transpose(t + 1)
+            if t < ROUNDS:
+                project(t)
+            if t >= 1:
+                sum_squares(t - 1)
+            if t + 1 < ROUNDS:
+                quantise(t + 1)
+            if t < ROUNDS:
+                add_bias(t)
+                if t % ROUNDS_PER_BATCH == ROUNDS_PER_BATCH - 1:
+                    store(t // ROUNDS_PER_BATCH, 2)
+            if t >= 1:
+                inverse_norms(t - 1)
+                scale(t - 1)
+                if (t - 1) % ROUNDS_PER_BATCH == ROUNDS_PER_BATCH - 1:
+                    store((t - 1) // ROUNDS_PER_BATCH, 0)
+                    store((t - 1) // ROUNDS_PER_BATCH, 1)

@@ -26,6 +26,7 @@ TILES = 4
 ROUNDS = BATCH * TOK_PER_PART // TILES
 ROUNDS_PER_BATCH = TOK_PER_PART // TILES
 X_BUFS = 8
+RUN_TILES = 2
 
 FLOPS = 2 * BATCH * SEQ * EMB * PROJ * FEAT
 
@@ -64,16 +65,19 @@ def tile_knnxlmultiheadsattention_pa_t_kernel(
             nc.sync.dma_start(out=x_sb[:], in_=x_view[b, :, half * TILES : (half + 1) * TILES, :])
             x_tiles[r] = x_sb
 
-        def transpose(r):
+        def transpose(r, tiles):
             x_words = x_tiles[r][:].rearrange("p i k -> p (i k)").bitcast(F32)
-            grouped = grouped_pool.tile([P, TILES, PASSES, P, PACK], BF16, align_bytes=64)
+            if tiles[0] == 0:
+                grouped = grouped_pool.tile([P, TILES, PASSES, P, PACK], BF16, align_bytes=64)
+                grouped_tiles[r] = grouped
+            grouped = grouped_tiles[r]
             grouped_words = (
                 grouped[:]
                 .rearrange("p i g w t -> p (i g w t)")
                 .bitcast(F32)
                 .rearrange("p (i g w u) -> p i g w u", i=TILES, g=PASSES, u=2)
             )
-            for i in range(TILES):
+            for i in tiles:
                 xt = xt_pool.tile([P, PASSES, 2, P], F32)
                 for g in range(PASSES):
                     first = (i * PASSES + g) * WORDS
@@ -84,8 +88,7 @@ def tile_knnxlmultiheadsattention_pa_t_kernel(
                     nc.scalar.copy(out=grouped_words[:, i], in_=planes_in_turn)
                 else:
                     nc.vector.tensor_copy(out=grouped_words[:, i], in_=planes_in_turn)
-            grouped_tiles[r] = grouped
-            if r + X_BUFS < ROUNDS:
+            if tiles[-1] == TILES - 1 and r + X_BUFS < ROUNDS:
                 load(r + X_BUFS)
 
         def quantise(r):
@@ -99,10 +102,10 @@ def tile_knnxlmultiheadsattention_pa_t_kernel(
             code_tiles[r] = codes
             plane_tiles[r] = planes
 
-        def project(r):
+        def project(r, tiles):
             codes = code_tiles[r]
             planes = plane_tiles[r]
-            for i in range(TILES):
+            for i in tiles:
                 acc = acc_pool.tile([P, 512], F32)
                 for cols in (slice(0, 2 * FEAT), slice(2 * FEAT, 3 * FEAT)):
                     for g in range(PASSES):
@@ -199,13 +202,14 @@ def tile_knnxlmultiheadsattention_pa_t_kernel(
         for r in range(2, X_BUFS):
             load(r)
 
-        transpose(0)
+        transpose(0, range(TILES))
         quantise(0)
         for t in range(ROUNDS + 1):
-            if t + 1 < ROUNDS:
-                transpose(t + 1)
-            if t < ROUNDS:
-                project(t)
+            for first in range(0, TILES, RUN_TILES):
+                if t + 1 < ROUNDS:
+                    transpose(t + 1, range(first, first + RUN_TILES))
+                if t < ROUNDS:
+                    project(t, range(first, first + RUN_TILES))
             if t >= 1:
                 sum_squares(t - 1)
             if t + 1 < ROUNDS:

@@ -26,7 +26,6 @@ TILES = 4
 ROUNDS = BATCH * TOK_PER_PART // TILES
 ROUNDS_PER_BATCH = TOK_PER_PART // TILES
 X_BUFS = 8
-RUN_TILES = 2
 
 FLOPS = 2 * BATCH * SEQ * EMB * PROJ * FEAT
 
@@ -65,19 +64,16 @@ def tile_knnxlmultiheadsattention_pa_t_kernel(
             nc.sync.dma_start(out=x_sb[:], in_=x_view[b, :, half * TILES : (half + 1) * TILES, :])
             x_tiles[r] = x_sb
 
-        def transpose(r, tiles):
+        def transpose(r):
             x_words = x_tiles[r][:].rearrange("p i k -> p (i k)").bitcast(F32)
-            if tiles[0] == 0:
-                grouped = grouped_pool.tile([P, TILES, PASSES, P, PACK], BF16, align_bytes=64)
-                grouped_tiles[r] = grouped
-            grouped = grouped_tiles[r]
+            grouped = grouped_pool.tile([P, TILES, PASSES, P, PACK], BF16, align_bytes=64)
             grouped_words = (
                 grouped[:]
                 .rearrange("p i g w t -> p (i g w t)")
                 .bitcast(F32)
                 .rearrange("p (i g w u) -> p i g w u", i=TILES, g=PASSES, u=2)
             )
-            for i in tiles:
+            for i in range(TILES):
                 xt = xt_pool.tile([P, PASSES, 2, P], F32)
                 for g in range(PASSES):
                     first = (i * PASSES + g) * WORDS
@@ -88,7 +84,8 @@ def tile_knnxlmultiheadsattention_pa_t_kernel(
                     nc.scalar.copy(out=grouped_words[:, i], in_=planes_in_turn)
                 else:
                     nc.vector.tensor_copy(out=grouped_words[:, i], in_=planes_in_turn)
-            if tiles[-1] == TILES - 1 and r + X_BUFS < ROUNDS:
+            grouped_tiles[r] = grouped
+            if r + X_BUFS < ROUNDS:
                 load(r + X_BUFS)
 
         def quantise(r):
@@ -102,10 +99,10 @@ def tile_knnxlmultiheadsattention_pa_t_kernel(
             code_tiles[r] = codes
             plane_tiles[r] = planes
 
-        def project(r, tiles):
+        def project(r):
             codes = code_tiles[r]
             planes = plane_tiles[r]
-            for i in tiles:
+            for i in range(TILES):
                 acc = acc_pool.tile([P, 512], F32)
                 for cols in (slice(0, 2 * FEAT), slice(2 * FEAT, 3 * FEAT)):
                     for g in range(PASSES):
@@ -148,15 +145,13 @@ def tile_knnxlmultiheadsattention_pa_t_kernel(
                         func=ACT.Square,
                         accum_out=sumsq[:, w, i : i + 1],
                     )
-            norm = small_pool.tile([P, 2, TILES], F32)
-            nc.scalar.sqrt(norm[:], sumsq[:])
-            norm_tiles[r] = norm
+            rnorm = small_pool.tile([P, 2, TILES], F32)
+            nc.scalar.activation(out=rnorm[:], in_=sumsq[:], func=ACT.Abs_reciprocal_sqrt)
+            norm_tiles[r] = rnorm
 
         def inverse_norms(r):
-            floored = small_pool.tile([P, 2, TILES], F32)
             inv = small_pool.tile([P, 2, TILES], F32)
-            nc.vector.tensor_scalar_max(floored[:], norm_tiles[r][:], 1e-12)
-            nc.vector.reciprocal(inv[:], floored[:])
+            nc.gpsimd.tensor_scalar_min(inv[:], norm_tiles[r][:], 1e12)
             inv_tiles[r] = inv
 
         def scale(r):
@@ -185,7 +180,7 @@ def tile_knnxlmultiheadsattention_pa_t_kernel(
         nc.vector.memset(w_planes[:].rearrange("p g n -> p (g n)").bitcast(I32), 0)
         warm = const.tile([P, 1], F32)
         nc.vector.memset(warm[:], 1.0)
-        nc.scalar.sqrt(warm[:], warm[:])
+        nc.scalar.activation(out=warm[:], in_=warm[:], func=ACT.Abs_reciprocal_sqrt)
 
         for w, (words, scales, bias) in enumerate(weights):
             cols = slice(w * FEAT, (w + 1) * FEAT)
@@ -202,14 +197,13 @@ def tile_knnxlmultiheadsattention_pa_t_kernel(
         for r in range(2, X_BUFS):
             load(r)
 
-        transpose(0, range(TILES))
+        transpose(0)
         quantise(0)
         for t in range(ROUNDS + 1):
-            for first in range(0, TILES, RUN_TILES):
-                if t + 1 < ROUNDS:
-                    transpose(t + 1, range(first, first + RUN_TILES))
-                if t < ROUNDS:
-                    project(t, range(first, first + RUN_TILES))
+            if t + 1 < ROUNDS:
+                transpose(t + 1)
+            if t < ROUNDS:
+                project(t)
             if t >= 1:
                 sum_squares(t - 1)
             if t + 1 < ROUNDS:

@@ -26,6 +26,7 @@ TILES = 4
 ROUNDS = BATCH * TOK_PER_PART // TILES
 ROUNDS_PER_BATCH = TOK_PER_PART // TILES
 X_BUFS = 8
+FINE_ROUNDS = 2
 
 FLOPS = 2 * BATCH * SEQ * EMB * PROJ * FEAT
 
@@ -44,7 +45,7 @@ def tile_knnxlmultiheadsattention_pa_t_kernel(
         x_pool = ctx.enter_context(tc.tile_pool(name="x", bufs=X_BUFS))
         grouped_pool = ctx.enter_context(tc.tile_pool(name="grouped", bufs=2))
         mx_pool = ctx.enter_context(tc.tile_pool(name="mx", bufs=2))
-        stage_pool = ctx.enter_context(tc.tile_pool(name="stage", bufs=3))
+        stage_pool = ctx.enter_context(tc.tile_pool(name="stage", bufs=4))
         small_pool = ctx.enter_context(tc.tile_pool(name="small", bufs=3))
         xt_pool = ctx.enter_context(tc.psum_pool(name="xt", bufs=TILES))
         acc_pool = ctx.enter_context(tc.psum_pool(name="acc", bufs=TILES))
@@ -56,12 +57,13 @@ def tile_knnxlmultiheadsattention_pa_t_kernel(
         acc_tiles = {}
         stage_tiles = {}
         norm_tiles = {}
-        inv_tiles = {}
 
         def load(r):
             b, half = divmod(r, ROUNDS_PER_BATCH)
             x_sb = x_pool.tile([P, TILES, EMB], BF16)
-            nc.sync.dma_start(out=x_sb[:], in_=x_view[b, :, half * TILES : (half + 1) * TILES, :])
+            step = 1 if r < FINE_ROUNDS else TILES
+            for i in range(0, TILES, step):
+                nc.sync.dma_start(out=x_sb[:, i : i + step, :], in_=x_view[b, :, half * TILES + i : half * TILES + i + step, :])
             x_tiles[r] = x_sb
 
         def transpose(r):
@@ -119,29 +121,25 @@ def tile_knnxlmultiheadsattention_pa_t_kernel(
                 acc_tiles[(r, i)] = acc
 
         def add_bias(r):
-            b, half = divmod(r, ROUNDS_PER_BATCH)
-            if half == 0:
-                stage = stage_pool.tile([P, PROJ, HEADS, TOK_PER_PART, HEAD_DIM], F32)
-                stage_tiles[b] = stage
-            stage = stage_tiles[b]
+            stage = stage_pool.tile([P, PROJ, HEADS, TILES, HEAD_DIM], F32)
+            stage_tiles[r] = stage
             for i in range(TILES):
                 nc.vector.tensor_tensor(
-                    out=stage[:, :, :, half * TILES + i, :],
+                    out=stage[:, :, :, i, :],
                     in0=acc_tiles[(r, i)][:, 0 : PROJ * FEAT].rearrange("p (w h d) -> p w h d", w=PROJ, h=HEADS),
                     in1=bias_bc[:].rearrange("p (w h d) -> p w h d", w=PROJ, h=HEADS),
                     op=ALU.add,
                 )
 
         def sum_squares(r):
-            b, half = divmod(r, ROUNDS_PER_BATCH)
-            stage = stage_tiles[b]
+            stage = stage_tiles[r]
             squares = small_pool.tile([P, 2, TILES, HEADS, HEAD_DIM], BF16)
             sumsq = small_pool.tile([P, 2, TILES], F32)
             for i in range(TILES):
                 for w in range(2):
                     nc.scalar.activation(
                         out=squares[:, w, i],
-                        in_=stage[:, w, :, half * TILES + i, :],
+                        in_=stage[:, w, :, i, :],
                         func=ACT.Square,
                         accum_out=sumsq[:, w, i : i + 1],
                     )
@@ -149,28 +147,22 @@ def tile_knnxlmultiheadsattention_pa_t_kernel(
             nc.scalar.activation(out=rnorm[:], in_=sumsq[:], func=ACT.Abs_reciprocal_sqrt)
             norm_tiles[r] = rnorm
 
-        def inverse_norms(r):
+        def scale(r, engine):
             inv = small_pool.tile([P, 2, TILES], F32)
-            nc.gpsimd.tensor_scalar_min(inv[:], norm_tiles[r][:], 1e12)
-            inv_tiles[r] = inv
-
-        def scale(r):
-            b, half = divmod(r, ROUNDS_PER_BATCH)
-            stage = stage_tiles[b]
+            engine.tensor_scalar_min(inv[:], norm_tiles[r][:], 1e12)
             for w in range(2):
-                part = stage[:, w, :, half * TILES : (half + 1) * TILES, :]
-                nc.gpsimd.tensor_tensor(
-                    out=part,
-                    in0=part,
-                    in1=inv_tiles[r][:, w, :].unsqueeze(1).unsqueeze(3).to_broadcast([P, HEADS, TILES, HEAD_DIM]),
+                engine.tensor_tensor(
+                    out=stage_tiles[r][:, w],
+                    in0=stage_tiles[r][:, w],
+                    in1=inv[:, w, :].unsqueeze(1).unsqueeze(3).to_broadcast([P, HEADS, TILES, HEAD_DIM]),
                     op=ALU.mult,
                 )
+                store(r, w)
 
-        def store(b, w):
-            nc.sync.dma_start(
-                out=outs[w][b].rearrange("h (p j) d -> p h (j d)", j=TOK_PER_PART),
-                in_=stage_tiles[b][:, w].rearrange("p h j d -> p h (j d)"),
-            )
+        def store(r, w):
+            b, half = divmod(r, ROUNDS_PER_BATCH)
+            out_view = outs[w][b].rearrange("h (p j) d -> p h j d", j=TOK_PER_PART)
+            nc.sync.dma_start(out=out_view[:, :, half * TILES : (half + 1) * TILES, :], in_=stage_tiles[r][:, w])
 
         ident = const.tile([P, P], F32)
         make_identity(nc, ident[:])
@@ -210,11 +202,6 @@ def tile_knnxlmultiheadsattention_pa_t_kernel(
                 quantise(t + 1)
             if t < ROUNDS:
                 add_bias(t)
-                if t % ROUNDS_PER_BATCH == ROUNDS_PER_BATCH - 1:
-                    store(t // ROUNDS_PER_BATCH, 2)
+                store(t, 2)
             if t >= 1:
-                inverse_norms(t - 1)
-                scale(t - 1)
-                if (t - 1) % ROUNDS_PER_BATCH == ROUNDS_PER_BATCH - 1:
-                    store((t - 1) // ROUNDS_PER_BATCH, 0)
-                    store((t - 1) // ROUNDS_PER_BATCH, 1)
+                scale(t - 1, nc.gpsimd if t < ROUNDS else nc.vector)

@@ -45,7 +45,7 @@ def tile_knnxlmultiheadsattention_pa_t_kernel(
         x_pool = ctx.enter_context(tc.tile_pool(name="x", bufs=X_BUFS))
         grouped_pool = ctx.enter_context(tc.tile_pool(name="grouped", bufs=2))
         mx_pool = ctx.enter_context(tc.tile_pool(name="mx", bufs=2))
-        stage_pool = ctx.enter_context(tc.tile_pool(name="stage", bufs=4))
+        stage_pool = ctx.enter_context(tc.tile_pool(name="stage", bufs=3))
         small_pool = ctx.enter_context(tc.tile_pool(name="small", bufs=3))
         xt_pool = ctx.enter_context(tc.psum_pool(name="xt", bufs=TILES))
         acc_pool = ctx.enter_context(tc.psum_pool(name="acc", bufs=TILES))
@@ -82,10 +82,10 @@ def tile_knnxlmultiheadsattention_pa_t_kernel(
                     for u in range(2):
                         nc.tensor.transpose(xt[:, g, u, :], x_words[:, first + u : first + WORDS : 2], ident[:])
                 planes_in_turn = xt[:].rearrange("p g u w -> p g w u")
-                if i < TILES - 1:
-                    nc.scalar.copy(out=grouped_words[:, i], in_=planes_in_turn)
-                else:
+                if i == 0:
                     nc.vector.tensor_copy(out=grouped_words[:, i], in_=planes_in_turn)
+                else:
+                    nc.scalar.copy(out=grouped_words[:, i], in_=planes_in_turn)
             grouped_tiles[r] = grouped
             if r + X_BUFS < ROUNDS:
                 load(r + X_BUFS)
@@ -121,25 +121,29 @@ def tile_knnxlmultiheadsattention_pa_t_kernel(
                 acc_tiles[(r, i)] = acc
 
         def add_bias(r):
-            stage = stage_pool.tile([P, PROJ, HEADS, TILES, HEAD_DIM], F32)
-            stage_tiles[r] = stage
+            b, half = divmod(r, ROUNDS_PER_BATCH)
+            if half == 0:
+                stage = stage_pool.tile([P, PROJ, HEADS, TOK_PER_PART, HEAD_DIM], F32)
+                stage_tiles[b] = stage
+            stage = stage_tiles[b]
             for i in range(TILES):
                 nc.vector.tensor_tensor(
-                    out=stage[:, :, :, i, :],
+                    out=stage[:, :, :, half * TILES + i, :],
                     in0=acc_tiles[(r, i)][:, 0 : PROJ * FEAT].rearrange("p (w h d) -> p w h d", w=PROJ, h=HEADS),
                     in1=bias_bc[:].rearrange("p (w h d) -> p w h d", w=PROJ, h=HEADS),
                     op=ALU.add,
                 )
 
         def sum_squares(r):
-            stage = stage_tiles[r]
+            b, half = divmod(r, ROUNDS_PER_BATCH)
+            stage = stage_tiles[b]
             squares = small_pool.tile([P, 2, TILES, HEADS, HEAD_DIM], BF16)
             sumsq = small_pool.tile([P, 2, TILES], F32)
             for i in range(TILES):
                 for w in range(2):
                     nc.scalar.activation(
                         out=squares[:, w, i],
-                        in_=stage[:, w, :, i, :],
+                        in_=stage[:, w, :, half * TILES + i, :],
                         func=ACT.Square,
                         accum_out=sumsq[:, w, i : i + 1],
                     )
@@ -148,21 +152,23 @@ def tile_knnxlmultiheadsattention_pa_t_kernel(
             norm_tiles[r] = rnorm
 
         def scale(r, engine):
+            b, half = divmod(r, ROUNDS_PER_BATCH)
             inv = small_pool.tile([P, 2, TILES], F32)
             engine.tensor_scalar_min(inv[:], norm_tiles[r][:], 1e12)
             for w in range(2):
+                part = stage_tiles[b][:, w, :, half * TILES : (half + 1) * TILES, :]
                 engine.tensor_tensor(
-                    out=stage_tiles[r][:, w],
-                    in0=stage_tiles[r][:, w],
+                    out=part,
+                    in0=part,
                     in1=inv[:, w, :].unsqueeze(1).unsqueeze(3).to_broadcast([P, HEADS, TILES, HEAD_DIM]),
                     op=ALU.mult,
                 )
-                store(r, w)
 
-        def store(r, w):
-            b, half = divmod(r, ROUNDS_PER_BATCH)
-            out_view = outs[w][b].rearrange("h (p j) d -> p h j d", j=TOK_PER_PART)
-            nc.sync.dma_start(out=out_view[:, :, half * TILES : (half + 1) * TILES, :], in_=stage_tiles[r][:, w])
+        def store(b, w):
+            nc.sync.dma_start(
+                out=outs[w][b].rearrange("h (p j) d -> p h (j d)", j=TOK_PER_PART),
+                in_=stage_tiles[b][:, w].rearrange("p h j d -> p h (j d)"),
+            )
 
         ident = const.tile([P, P], F32)
         make_identity(nc, ident[:])
@@ -202,6 +208,10 @@ def tile_knnxlmultiheadsattention_pa_t_kernel(
                 quantise(t + 1)
             if t < ROUNDS:
                 add_bias(t)
-                store(t, 2)
+                if t % ROUNDS_PER_BATCH == ROUNDS_PER_BATCH - 1:
+                    store(t // ROUNDS_PER_BATCH, 2)
             if t >= 1:
                 scale(t - 1, nc.gpsimd if t < ROUNDS else nc.vector)
+                if (t - 1) % ROUNDS_PER_BATCH == ROUNDS_PER_BATCH - 1:
+                    store((t - 1) // ROUNDS_PER_BATCH, 0)
+                    store((t - 1) // ROUNDS_PER_BATCH, 1)

@@ -175,11 +175,17 @@ def tile_knnxlmultiheadsattention_pa_t_kernel(
         w_codes = const.tile([P, PASSES, PROJ * FEAT], U32, align_bytes=64)
         w_planes = const.tile([P, PASSES, PROJ * FEAT], U8, align_bytes=64)
         bias_bc = const.tile([P, PROJ * FEAT], BF16)
+        bias_rows = const.tile([P, PROJ * FEAT], BF16)
+        ones = const.tile([P, P], BF16)
+        nc.vector.memset(bias_rows[:], 0.0)
+        nc.vector.memset(ones[:], 1.0)
         nc.vector.memset(w_planes[:].rearrange("p g n -> p (g n)").bitcast(I32), 0)
         warm = const.tile([P, 1], F32)
         nc.vector.memset(warm[:], 1.0)
         nc.scalar.activation(out=warm[:], in_=warm[:], func=ACT.Abs_reciprocal_sqrt)
 
+        for w, (words, scales, bias) in enumerate(weights):
+            nc.scalar.dma_start(out=bias_rows[0:1, w * FEAT : (w + 1) * FEAT], in_=bias.rearrange("(o n) -> o n", o=1))
         for w, (words, scales, bias) in enumerate(weights):
             cols = slice(w * FEAT, (w + 1) * FEAT)
             nc.sync.dma_start(
@@ -188,15 +194,14 @@ def tile_knnxlmultiheadsattention_pa_t_kernel(
             rows = scales.bitcast(I32).rearrange("g (q r) n -> r q g n", r=4)
             for r in range(4):
                 nc.sync.dma_start(out=w_planes[r:P:32, :, cols].bitcast(I32), in_=rows[r])
-        load(0)
-        load(1)
-        for w, (words, scales, bias) in enumerate(weights):
-            nc.sync.dma_start(out=bias_bc[:, w * FEAT : (w + 1) * FEAT], in_=bias.partition_broadcast(P))
-        for r in range(2, X_BUFS):
+        for r in range(X_BUFS):
             load(r)
 
         transpose(0)
         quantise(0)
+        acc = acc_pool.tile([P, 512], F32)
+        nc.tensor.matmul(out=acc[:, 0 : PROJ * FEAT], lhsT=ones[:], rhs=bias_rows[:], start=True, stop=True)
+        nc.vector.tensor_copy(out=bias_bc[:], in_=acc[:, 0 : PROJ * FEAT])
         for t in range(ROUNDS + 1):
             if t + 1 < ROUNDS:
                 transpose(t + 1)

@@ -177,15 +177,13 @@ def tile_knnxlmultiheadsattention_pa_t_kernel(
         bias_bc = const.tile([P, PROJ * FEAT], BF16)
         bias_rows = const.tile([P, PROJ * FEAT], BF16)
         ones = const.tile([P, P], BF16)
+        nc.vector.memset(w_planes[:].rearrange("p g n -> p (g n)").bitcast(I32), 0)
         nc.vector.memset(bias_rows[:], 0.0)
         nc.vector.memset(ones[:], 1.0)
-        nc.vector.memset(w_planes[:].rearrange("p g n -> p (g n)").bitcast(I32), 0)
         warm = const.tile([P, 1], F32)
         nc.vector.memset(warm[:], 1.0)
         nc.scalar.activation(out=warm[:], in_=warm[:], func=ACT.Abs_reciprocal_sqrt)
 
-        for w, (words, scales, bias) in enumerate(weights):
-            nc.scalar.dma_start(out=bias_rows[0:1, w * FEAT : (w + 1) * FEAT], in_=bias.rearrange("(o n) -> o n", o=1))
         for w, (words, scales, bias) in enumerate(weights):
             cols = slice(w * FEAT, (w + 1) * FEAT)
             nc.sync.dma_start(
@@ -194,17 +192,22 @@ def tile_knnxlmultiheadsattention_pa_t_kernel(
             rows = scales.bitcast(I32).rearrange("g (q r) n -> r q g n", r=4)
             for r in range(4):
                 nc.sync.dma_start(out=w_planes[r:P:32, :, cols].bitcast(I32), in_=rows[r])
-        for r in range(X_BUFS):
+        load(0)
+        load(1)
+        for w, (words, scales, bias) in enumerate(weights):
+            nc.sync.dma_start(out=bias_rows[0:1, w * FEAT : (w + 1) * FEAT], in_=bias.rearrange("(o n) -> o n", o=1))
+        for r in range(2, X_BUFS):
             load(r)
 
         transpose(0)
         quantise(0)
-        acc = acc_pool.tile([P, 512], F32)
-        nc.tensor.matmul(out=acc[:, 0 : PROJ * FEAT], lhsT=ones[:], rhs=bias_rows[:], start=True, stop=True)
-        nc.vector.tensor_copy(out=bias_bc[:], in_=acc[:, 0 : PROJ * FEAT])
         for t in range(ROUNDS + 1):
             if t + 1 < ROUNDS:
                 transpose(t + 1)
+            if t == 0:
+                acc = acc_pool.tile([P, 512], F32)
+                nc.tensor.matmul(out=acc[:, 0 : PROJ * FEAT], lhsT=ones[:], rhs=bias_rows[:], start=True, stop=True)
+                nc.vector.tensor_copy(out=bias_bc[:], in_=acc[:, 0 : PROJ * FEAT])
             if t < ROUNDS:
                 project(t)
             if t >= 1:

@@ -27,6 +27,7 @@ ROUNDS = BATCH * TOK_PER_PART // TILES
 ROUNDS_PER_BATCH = TOK_PER_PART // TILES
 X_BUFS = 8
 FINE_ROUNDS = 2
+END_TILES = 2
 
 FLOPS = 2 * BATCH * SEQ * EMB * PROJ * FEAT
 
@@ -81,11 +82,7 @@ def tile_knnxlmultiheadsattention_pa_t_kernel(
                     first = (i * PASSES + g) * WORDS
                     for u in range(2):
                         nc.tensor.transpose(xt[:, g, u, :], x_words[:, first + u : first + WORDS : 2], ident[:])
-                planes_in_turn = xt[:].rearrange("p g u w -> p g w u")
-                if i == 0:
-                    nc.vector.tensor_copy(out=grouped_words[:, i], in_=planes_in_turn)
-                else:
-                    nc.scalar.copy(out=grouped_words[:, i], in_=planes_in_turn)
+                nc.scalar.copy(out=grouped_words[:, i], in_=xt[:].rearrange("p g u w -> p g w u"))
             grouped_tiles[r] = grouped
             if r + X_BUFS < ROUNDS:
                 load(r + X_BUFS)
@@ -151,24 +148,54 @@ def tile_knnxlmultiheadsattention_pa_t_kernel(
             nc.scalar.activation(out=rnorm[:], in_=sumsq[:], func=ACT.Abs_reciprocal_sqrt)
             norm_tiles[r] = rnorm
 
-        def scale(r, engine):
+        def scale(r, engines):
             b, half = divmod(r, ROUNDS_PER_BATCH)
             inv = small_pool.tile([P, 2, TILES], F32)
-            engine.tensor_scalar_min(inv[:], norm_tiles[r][:], 1e12)
+            engines[0].tensor_scalar_min(inv[:], norm_tiles[r][:], 1e12)
             for w in range(2):
                 part = stage_tiles[b][:, w, :, half * TILES : (half + 1) * TILES, :]
-                engine.tensor_tensor(
+                engines[w].tensor_tensor(
                     out=part,
                     in0=part,
                     in1=inv[:, w, :].unsqueeze(1).unsqueeze(3).to_broadcast([P, HEADS, TILES, HEAD_DIM]),
                     op=ALU.mult,
                 )
 
-        def store(b, w):
+        def store(b, w, first=0, count=TOK_PER_PART):
+            run = slice(first * HEAD_DIM, (first + count) * HEAD_DIM)
             nc.sync.dma_start(
-                out=outs[w][b].rearrange("h (p j) d -> p h (j d)", j=TOK_PER_PART),
-                in_=stage_tiles[b][:, w].rearrange("p h j d -> p h (j d)"),
+                out=outs[w][b].rearrange("h (p j) d -> p h (j d)", j=TOK_PER_PART)[:, :, run],
+                in_=stage_tiles[b][:, w].rearrange("p h j d -> p h (j d)")[:, :, run],
             )
+
+        def finish(r):
+            b, half = divmod(r, ROUNDS_PER_BATCH)
+            stage = stage_tiles[b]
+            squares = small_pool.tile([P, 2, TILES, HEADS, HEAD_DIM], BF16)
+            sumsq = small_pool.tile([P, 2, TILES], F32)
+            rnorm = small_pool.tile([P, 2, TILES], F32)
+            inv = small_pool.tile([P, 2, TILES], F32)
+            for lo in range(0, TILES, END_TILES):
+                some = slice(lo, lo + END_TILES)
+                for i in range(lo, lo + END_TILES):
+                    for w in range(2):
+                        nc.scalar.activation(
+                            out=squares[:, w, i],
+                            in_=stage[:, w, :, half * TILES + i, :],
+                            func=ACT.Square,
+                            accum_out=sumsq[:, w, i : i + 1],
+                        )
+                nc.scalar.activation(out=rnorm[:, :, some], in_=sumsq[:, :, some], func=ACT.Abs_reciprocal_sqrt)
+                nc.vector.tensor_scalar_min(inv[:, :, some], rnorm[:, :, some], 1e12)
+                for w in range(2):
+                    part = stage[:, w, :, half * TILES + lo : half * TILES + lo + END_TILES, :]
+                    nc.vector.tensor_tensor(
+                        out=part,
+                        in0=part,
+                        in1=inv[:, w, some].unsqueeze(1).unsqueeze(3).to_broadcast([P, HEADS, END_TILES, HEAD_DIM]),
+                        op=ALU.mult,
+                    )
+                    store(b, w, half * TILES + lo, END_TILES)
 
         ident = const.tile([P, P], F32)
         make_identity(nc, ident[:])
@@ -210,16 +237,23 @@ def tile_knnxlmultiheadsattention_pa_t_kernel(
                 nc.vector.tensor_copy(out=bias_bc[:], in_=acc[:, 0 : PROJ * FEAT])
             if t < ROUNDS:
                 project(t)
-            if t >= 1:
+            if 1 <= t < ROUNDS:
                 sum_squares(t - 1)
             if t + 1 < ROUNDS:
                 quantise(t + 1)
             if t < ROUNDS:
                 add_bias(t)
-                if t % ROUNDS_PER_BATCH == ROUNDS_PER_BATCH - 1:
-                    store(t // ROUNDS_PER_BATCH, 2)
-            if t >= 1:
-                scale(t - 1, nc.gpsimd if t < ROUNDS else nc.vector)
-                if (t - 1) % ROUNDS_PER_BATCH == ROUNDS_PER_BATCH - 1:
-                    store((t - 1) // ROUNDS_PER_BATCH, 0)
-                    store((t - 1) // ROUNDS_PER_BATCH, 1)
+                b, half = divmod(t, ROUNDS_PER_BATCH)
+                if b == BATCH - 1:
+                    store(b, 2, half * TILES, TILES)
+                elif half == ROUNDS_PER_BATCH - 1:
+                    store(b, 2)
+            if 1 <= t < ROUNDS:
+                scale(t - 1, (nc.gpsimd, nc.vector))
+                b, half = divmod(t - 1, ROUNDS_PER_BATCH)
+                for w in range(2):
+                    if b == BATCH - 1:
+                        store(b, w, half * TILES, TILES)
+                    elif half == ROUNDS_PER_BATCH - 1:
+                        store(b, w)
+        finish(ROUNDS - 1)

@@ -27,6 +27,7 @@ ROUNDS = BATCH * TOK_PER_PART // TILES
 ROUNDS_PER_BATCH = TOK_PER_PART // TILES
 X_BUFS = 8
 FINE_ROUNDS = 2
+SORTED = 1
 END_TILES = 2
 
 FLOPS = 2 * BATCH * SEQ * EMB * PROJ * FEAT
@@ -44,6 +45,7 @@ def tile_knnxlmultiheadsattention_pa_t_kernel(
         ctx.enter_context(tc.manual_schedule())
         const = ctx.enter_context(tc.tile_pool(name="const", bufs=1))
         x_pool = ctx.enter_context(tc.tile_pool(name="x", bufs=X_BUFS))
+        sorted_pool = ctx.enter_context(tc.tile_pool(name="sorted", bufs=3))
         grouped_pool = ctx.enter_context(tc.tile_pool(name="grouped", bufs=2))
         mx_pool = ctx.enter_context(tc.tile_pool(name="mx", bufs=2))
         stage_pool = ctx.enter_context(tc.tile_pool(name="stage", bufs=3))
@@ -52,6 +54,7 @@ def tile_knnxlmultiheadsattention_pa_t_kernel(
         acc_pool = ctx.enter_context(tc.psum_pool(name="acc", bufs=TILES))
 
         x_tiles = {}
+        sorted_tiles = {}
         grouped_tiles = {}
         code_tiles = {}
         plane_tiles = {}
@@ -67,6 +70,14 @@ def tile_knnxlmultiheadsattention_pa_t_kernel(
                 nc.sync.dma_start(out=x_sb[:, i : i + step, :], in_=x_view[b, :, half * TILES + i : half * TILES + i + step, :])
             x_tiles[r] = x_sb
 
+        def sort_words(r):
+            x_words = x_tiles[r][:].rearrange("p i k -> p (i k)").bitcast(F32)
+            in_order = sorted_pool.tile([P, SORTED * PASSES, 2, P], F32)
+            nc.vector.tensor_copy(
+                out=in_order[:], in_=x_words[:, 0 : SORTED * PASSES * WORDS].rearrange("p (a w u) -> p a u w", w=P, u=2)
+            )
+            sorted_tiles[r] = in_order
+
         def transpose(r):
             x_words = x_tiles[r][:].rearrange("p i k -> p (i k)").bitcast(F32)
             grouped = grouped_pool.tile([P, TILES, PASSES, P, PACK], BF16, align_bytes=64)
@@ -81,7 +92,10 @@ def tile_knnxlmultiheadsattention_pa_t_kernel(
                 for g in range(PASSES):
                     first = (i * PASSES + g) * WORDS
                     for u in range(2):
-                        nc.tensor.transpose(xt[:, g, u, :], x_words[:, first + u : first + WORDS : 2], ident[:])
+                        if i < SORTED:
+                            nc.tensor.transpose(xt[:, g, u, :], sorted_tiles[r][:, i * PASSES + g, u, :], ident[:])
+                        else:
+                            nc.tensor.transpose(xt[:, g, u, :], x_words[:, first + u : first + WORDS : 2], ident[:])
                 nc.scalar.copy(out=grouped_words[:, i], in_=xt[:].rearrange("p g u w -> p g w u"))
             grouped_tiles[r] = grouped
             if r + X_BUFS < ROUNDS:
@@ -226,8 +240,11 @@ def tile_knnxlmultiheadsattention_pa_t_kernel(
         for r in range(2, X_BUFS):
             load(r)
 
+        sort_words(0)
         transpose(0)
+        sort_words(1)
         quantise(0)
+        sort_words(2)
         for t in range(ROUNDS + 1):
             if t + 1 < ROUNDS:
                 transpose(t + 1)
@@ -241,6 +258,8 @@ def tile_knnxlmultiheadsattention_pa_t_kernel(
                 sum_squares(t - 1)
             if t + 1 < ROUNDS:
                 quantise(t + 1)
+            if t + 3 < ROUNDS:
+                sort_words(t + 3)
             if t < ROUNDS:
                 add_bias(t)
                 b, half = divmod(t, ROUNDS_PER_BATCH)

@@ -61,6 +61,7 @@ def tile_knnxlmultiheadsattention_pa_t_kernel(
         acc_tiles = {}
         stage_tiles = {}
         norm_tiles = {}
+        inv_tiles = {}
 
         def load(r):
             b, half = divmod(r, ROUNDS_PER_BATCH)
@@ -131,13 +132,13 @@ def tile_knnxlmultiheadsattention_pa_t_kernel(
                         )
                 acc_tiles[(r, i)] = acc
 
-        def add_bias(r):
+        def add_bias(r, tiles):
             b, half = divmod(r, ROUNDS_PER_BATCH)
-            if half == 0:
+            if half == 0 and tiles[0] == 0:
                 stage = stage_pool.tile([P, PROJ, HEADS, TOK_PER_PART, HEAD_DIM], F32)
                 stage_tiles[b] = stage
             stage = stage_tiles[b]
-            for i in range(TILES):
+            for i in tiles:
                 nc.vector.tensor_tensor(
                     out=stage[:, :, :, half * TILES + i, :],
                     in0=acc_tiles[(r, i)][:, 0 : PROJ * FEAT].rearrange("p (w h d) -> p w h d", w=PROJ, h=HEADS),
@@ -162,18 +163,17 @@ def tile_knnxlmultiheadsattention_pa_t_kernel(
             nc.scalar.activation(out=rnorm[:], in_=sumsq[:], func=ACT.Abs_reciprocal_sqrt)
             norm_tiles[r] = rnorm
 
-        def scale(r, engines):
-            b, half = divmod(r, ROUNDS_PER_BATCH)
+        def floor_norms(r):
             inv = small_pool.tile([P, 2, TILES], F32)
-            engines[0].tensor_scalar_min(inv[:], norm_tiles[r][:], 1e12)
+            nc.vector.tensor_scalar_min(inv[:], norm_tiles[r][:], 1e12)
+            inv_tiles[r] = inv
+
+        def scale(r):
+            b, half = divmod(r, ROUNDS_PER_BATCH)
             for w in range(2):
-                part = stage_tiles[b][:, w, :, half * TILES : (half + 1) * TILES, :]
-                engines[w].tensor_tensor(
-                    out=part,
-                    in0=part,
-                    in1=inv[:, w, :].unsqueeze(1).unsqueeze(3).to_broadcast([P, HEADS, TILES, HEAD_DIM]),
-                    op=ALU.mult,
-                )
+                for i in range(TILES):
+                    part = stage_tiles[b][:, w, :, half * TILES + i, :]
+                    nc.vector.tensor_scalar_mul(part, part, inv_tiles[r][:, w, i : i + 1])
 
         def store(b, w, first=0, count=TOK_PER_PART):
             run = slice(first * HEAD_DIM, (first + count) * HEAD_DIM)
@@ -261,14 +261,17 @@ def tile_knnxlmultiheadsattention_pa_t_kernel(
             if t + 3 < ROUNDS:
                 sort_words(t + 3)
             if t < ROUNDS:
-                add_bias(t)
+                add_bias(t, range(TILES - 1))
+                if 1 <= t:
+                    floor_norms(t - 1)
+                add_bias(t, range(TILES - 1, TILES))
                 b, half = divmod(t, ROUNDS_PER_BATCH)
                 if b == BATCH - 1:
                     store(b, 2, half * TILES, TILES)
                 elif half == ROUNDS_PER_BATCH - 1:
                     store(b, 2)
             if 1 <= t < ROUNDS:
-                scale(t - 1, (nc.gpsimd, nc.vector))
+                scale(t - 1)
                 b, half = divmod(t - 1, ROUNDS_PER_BATCH)
                 for w in range(2):
                     if b == BATCH - 1:

@@ -26,7 +26,6 @@ TILES = 4
 ROUNDS = BATCH * TOK_PER_PART // TILES
 ROUNDS_PER_BATCH = TOK_PER_PART // TILES
 X_BUFS = 8
-FINE_ROUNDS = 2
 SORTED = 1
 END_TILES = 2
 
@@ -63,12 +62,11 @@ def tile_knnxlmultiheadsattention_pa_t_kernel(
         norm_tiles = {}
         inv_tiles = {}
 
-        def load(r):
+        def load(r, queue=nc.sync, step=TILES):
             b, half = divmod(r, ROUNDS_PER_BATCH)
             x_sb = x_pool.tile([P, TILES, EMB], BF16)
-            step = 1 if r < FINE_ROUNDS else TILES
             for i in range(0, TILES, step):
-                nc.sync.dma_start(out=x_sb[:, i : i + step, :], in_=x_view[b, :, half * TILES + i : half * TILES + i + step, :])
+                queue.dma_start(out=x_sb[:, i : i + step, :], in_=x_view[b, :, half * TILES + i : half * TILES + i + step, :])
             x_tiles[r] = x_sb
 
         def sort_words(r):
@@ -211,8 +209,11 @@ def tile_knnxlmultiheadsattention_pa_t_kernel(
                     )
                     store(b, w, half * TILES + lo, END_TILES)
 
+        load(0, nc.scalar, TILES // 2)
+
         ident = const.tile([P, P], F32)
         make_identity(nc, ident[:])
+        load(1, nc.gpsimd)
         w_codes = const.tile([P, PASSES, PROJ * FEAT], U32, align_bytes=64)
         w_planes = const.tile([P, PASSES, PROJ * FEAT], U8, align_bytes=64)
         bias_bc = const.tile([P, PROJ * FEAT], BF16)
@@ -230,11 +231,11 @@ def tile_knnxlmultiheadsattention_pa_t_kernel(
             nc.sync.dma_start(
                 out=w_codes[:, :, cols].bitcast(I32), in_=words.rearrange("g p n t -> p g (n t)").bitcast(I32)
             )
+        for w, (words, scales, bias) in enumerate(weights):
+            cols = slice(w * FEAT, (w + 1) * FEAT)
             rows = scales.bitcast(I32).rearrange("g (q r) n -> r q g n", r=4)
             for r in range(4):
                 nc.sync.dma_start(out=w_planes[r:P:32, :, cols].bitcast(I32), in_=rows[r])
-        load(0)
-        load(1)
         for w, (words, scales, bias) in enumerate(weights):
             nc.sync.dma_start(out=bias_rows[0:1, w * FEAT : (w + 1) * FEAT], in_=bias.rearrange("(o n) -> o n", o=1))
         for r in range(2, X_BUFS):

@@ -23,11 +23,11 @@ PASSES = EMB // K_PASS
 WORDS = K_PASS // 2
 TOK_PER_PART = SEQ // P
 TILES = 4
-ROUNDS = BATCH * TOK_PER_PART // TILES
-ROUNDS_PER_BATCH = TOK_PER_PART // TILES
+SIZES = (TILES,) * 15 + (2, 2)
+ROUNDS = len(SIZES)
 X_BUFS = 8
+FIRST_SORTED = 4
 SORTED = 1
-END_TILES = 2
 
 FLOPS = 2 * BATCH * SEQ * EMB * PROJ * FEAT
 
@@ -52,6 +52,7 @@ def tile_knnxlmultiheadsattention_pa_t_kernel(
         xt_pool = ctx.enter_context(tc.psum_pool(name="xt", bufs=TILES))
         acc_pool = ctx.enter_context(tc.psum_pool(name="acc", bufs=TILES))
 
+        starts = [divmod(sum(SIZES[:r]), TOK_PER_PART) for r in range(ROUNDS)]
         x_tiles = {}
         sorted_tiles = {}
         grouped_tiles = {}
@@ -62,11 +63,11 @@ def tile_knnxlmultiheadsattention_pa_t_kernel(
         norm_tiles = {}
         inv_tiles = {}
 
-        def load(r, queue=nc.sync, step=TILES):
-            b, half = divmod(r, ROUNDS_PER_BATCH)
+        def load(r, pieces=()):
+            b, j = starts[r]
             x_sb = x_pool.tile([P, TILES, EMB], BF16)
-            for i in range(0, TILES, step):
-                queue.dma_start(out=x_sb[:, i : i + step, :], in_=x_view[b, :, half * TILES + i : half * TILES + i + step, :])
+            for queue, lo, hi in pieces or ((nc.sync, 0, SIZES[r]),):
+                queue.dma_start(out=x_sb[:, lo:hi, :], in_=x_view[b, :, j + lo : j + hi, :])
             x_tiles[r] = x_sb
 
         def sort_words(r):
@@ -86,12 +87,12 @@ def tile_knnxlmultiheadsattention_pa_t_kernel(
                 .bitcast(F32)
                 .rearrange("p (i g w u) -> p i g w u", i=TILES, g=PASSES, u=2)
             )
-            for i in range(TILES):
+            for i in range(SIZES[r]):
                 xt = xt_pool.tile([P, PASSES, 2, P], F32)
                 for g in range(PASSES):
                     first = (i * PASSES + g) * WORDS
                     for u in range(2):
-                        if i < SORTED:
+                        if i < SORTED and r in sorted_tiles:
                             nc.tensor.transpose(xt[:, g, u, :], sorted_tiles[r][:, i * PASSES + g, u, :], ident[:])
                         else:
                             nc.tensor.transpose(xt[:, g, u, :], x_words[:, first + u : first + WORDS : 2], ident[:])
@@ -103,10 +104,11 @@ def tile_knnxlmultiheadsattention_pa_t_kernel(
         def quantise(r):
             codes = mx_pool.tile([P, TILES * PASSES * P], U32, align_bytes=64)
             planes = mx_pool.tile([P, TILES * PASSES * P], U8, align_bytes=64)
+            cols = SIZES[r] * PASSES * P
             nc.vector.quantize_mx(
-                out=codes[:].bitcast(FP8X4),
-                scales=planes[:],
-                in_=grouped_tiles[r][:].rearrange("p i g w t -> p (i g w t)"),
+                out=codes[:, 0:cols].bitcast(FP8X4),
+                scales=planes[:, 0:cols],
+                in_=grouped_tiles[r][:].rearrange("p i g w t -> p (i g w t)")[:, 0 : cols * PACK],
             )
             code_tiles[r] = codes
             plane_tiles[r] = planes
@@ -114,7 +116,7 @@ def tile_knnxlmultiheadsattention_pa_t_kernel(
         def project(r):
             codes = code_tiles[r]
             planes = plane_tiles[r]
-            for i in range(TILES):
+            for i in range(SIZES[r]):
                 acc = acc_pool.tile([P, 512], F32)
                 for cols in (slice(0, 2 * FEAT), slice(2 * FEAT, 3 * FEAT)):
                     for g in range(PASSES):
@@ -131,46 +133,48 @@ def tile_knnxlmultiheadsattention_pa_t_kernel(
                 acc_tiles[(r, i)] = acc
 
         def add_bias(r, tiles):
-            b, half = divmod(r, ROUNDS_PER_BATCH)
-            if half == 0 and tiles[0] == 0:
+            b, j = starts[r]
+            if j == 0 and b not in stage_tiles:
                 stage = stage_pool.tile([P, PROJ, HEADS, TOK_PER_PART, HEAD_DIM], F32)
                 stage_tiles[b] = stage
             stage = stage_tiles[b]
             for i in tiles:
                 nc.vector.tensor_tensor(
-                    out=stage[:, :, :, half * TILES + i, :],
+                    out=stage[:, :, :, j + i, :],
                     in0=acc_tiles[(r, i)][:, 0 : PROJ * FEAT].rearrange("p (w h d) -> p w h d", w=PROJ, h=HEADS),
                     in1=bias_bc[:].rearrange("p (w h d) -> p w h d", w=PROJ, h=HEADS),
                     op=ALU.add,
                 )
 
         def sum_squares(r):
-            b, half = divmod(r, ROUNDS_PER_BATCH)
+            b, j = starts[r]
             stage = stage_tiles[b]
             squares = small_pool.tile([P, 2, TILES, HEADS, HEAD_DIM], BF16)
             sumsq = small_pool.tile([P, 2, TILES], F32)
-            for i in range(TILES):
+            for i in range(SIZES[r]):
                 for w in range(2):
                     nc.scalar.activation(
                         out=squares[:, w, i],
-                        in_=stage[:, w, :, half * TILES + i, :],
+                        in_=stage[:, w, :, j + i, :],
                         func=ACT.Square,
                         accum_out=sumsq[:, w, i : i + 1],
                     )
             rnorm = small_pool.tile([P, 2, TILES], F32)
-            nc.scalar.activation(out=rnorm[:], in_=sumsq[:], func=ACT.Abs_reciprocal_sqrt)
+            some = slice(0, SIZES[r])
+            nc.scalar.activation(out=rnorm[:, :, some], in_=sumsq[:, :, some], func=ACT.Abs_reciprocal_sqrt)
             norm_tiles[r] = rnorm
 
         def floor_norms(r):
             inv = small_pool.tile([P, 2, TILES], F32)
-            nc.vector.tensor_scalar_min(inv[:], norm_tiles[r][:], 1e12)
+            some = slice(0, SIZES[r])
+            nc.vector.tensor_scalar_min(inv[:, :, some], norm_tiles[r][:, :, some], 1e12)
             inv_tiles[r] = inv
 
         def scale(r):
-            b, half = divmod(r, ROUNDS_PER_BATCH)
+            b, j = starts[r]
             for w in range(2):
-                for i in range(TILES):
-                    part = stage_tiles[b][:, w, :, half * TILES + i, :]
+                for i in range(SIZES[r]):
+                    part = stage_tiles[b][:, w, :, j + i, :]
                     nc.vector.tensor_scalar_mul(part, part, inv_tiles[r][:, w, i : i + 1])
 
         def store(b, w, first=0, count=TOK_PER_PART):
@@ -180,40 +184,19 @@ def tile_knnxlmultiheadsattention_pa_t_kernel(
                 in_=stage_tiles[b][:, w].rearrange("p h j d -> p h (j d)")[:, :, run],
             )
 
-        def finish(r):
-            b, half = divmod(r, ROUNDS_PER_BATCH)
-            stage = stage_tiles[b]
-            squares = small_pool.tile([P, 2, TILES, HEADS, HEAD_DIM], BF16)
-            sumsq = small_pool.tile([P, 2, TILES], F32)
-            rnorm = small_pool.tile([P, 2, TILES], F32)
-            inv = small_pool.tile([P, 2, TILES], F32)
-            for lo in range(0, TILES, END_TILES):
-                some = slice(lo, lo + END_TILES)
-                for i in range(lo, lo + END_TILES):
-                    for w in range(2):
-                        nc.scalar.activation(
-                            out=squares[:, w, i],
-                            in_=stage[:, w, :, half * TILES + i, :],
-                            func=ACT.Square,
-                            accum_out=sumsq[:, w, i : i + 1],
-                        )
-                nc.scalar.activation(out=rnorm[:, :, some], in_=sumsq[:, :, some], func=ACT.Abs_reciprocal_sqrt)
-                nc.vector.tensor_scalar_min(inv[:, :, some], rnorm[:, :, some], 1e12)
-                for w in range(2):
-                    part = stage[:, w, :, half * TILES + lo : half * TILES + lo + END_TILES, :]
-                    nc.vector.tensor_tensor(
-                        out=part,
-                        in0=part,
-                        in1=inv[:, w, some].unsqueeze(1).unsqueeze(3).to_broadcast([P, HEADS, END_TILES, HEAD_DIM]),
-                        op=ALU.mult,
-                    )
-                    store(b, w, half * TILES + lo, END_TILES)
+        def store_ready(r, parts):
+            b, j = starts[r]
+            for w in parts:
+                if b == BATCH - 1:
+                    store(b, w, j, SIZES[r])
+                elif j + SIZES[r] == TOK_PER_PART:
+                    store(b, w)
 
-        load(0, nc.scalar, TILES // 2)
+        load(0, ((nc.scalar, 0, 1), (nc.scalar, 1, 2), (nc.scalar, 2, TILES)))
 
         ident = const.tile([P, P], F32)
         make_identity(nc, ident[:])
-        load(1, nc.gpsimd)
+        load(1, ((nc.gpsimd, 0, 2), (nc.gpsimd, 2, TILES)))
         w_codes = const.tile([P, PASSES, PROJ * FEAT], U32, align_bytes=64)
         w_planes = const.tile([P, PASSES, PROJ * FEAT], U8, align_bytes=64)
         bias_bc = const.tile([P, PROJ * FEAT], BF16)
@@ -238,45 +221,36 @@ def tile_knnxlmultiheadsattention_pa_t_kernel(
                 nc.sync.dma_start(out=w_planes[r:P:32, :, cols].bitcast(I32), in_=rows[r])
         for w, (words, scales, bias) in enumerate(weights):
             nc.sync.dma_start(out=bias_rows[0:1, w * FEAT : (w + 1) * FEAT], in_=bias.rearrange("(o n) -> o n", o=1))
-        for r in range(2, X_BUFS):
+        load(2, ((nc.sync, 0, 2), (nc.sync, 2, TILES)))
+        for r in range(3, X_BUFS):
             load(r)
 
-        sort_words(0)
         transpose(0)
-        sort_words(1)
         quantise(0)
-        sort_words(2)
         for t in range(ROUNDS + 1):
             if t + 1 < ROUNDS:
                 transpose(t + 1)
-            if t == 0:
-                acc = acc_pool.tile([P, 512], F32)
-                nc.tensor.matmul(out=acc[:, 0 : PROJ * FEAT], lhsT=ones[:], rhs=bias_rows[:], start=True, stop=True)
-                nc.vector.tensor_copy(out=bias_bc[:], in_=acc[:, 0 : PROJ * FEAT])
             if t < ROUNDS:
                 project(t)
-            if 1 <= t < ROUNDS:
+            if t == 0:
+                xt = xt_pool.tile([P, PASSES, 2, P], F32)
+                spread = xt[:].rearrange("p g u w -> p (g u w)")[:, 0 : PROJ * FEAT]
+                nc.tensor.matmul(out=spread, lhsT=ones[:], rhs=bias_rows[:], start=True, stop=True)
+            if 1 <= t:
                 sum_squares(t - 1)
             if t + 1 < ROUNDS:
                 quantise(t + 1)
-            if t + 3 < ROUNDS:
+            if FIRST_SORTED <= t + 3 < ROUNDS and SIZES[t + 3] == TILES:
                 sort_words(t + 3)
+            if t == 0:
+                nc.vector.tensor_copy(out=bias_bc[:], in_=spread)
             if t < ROUNDS:
-                add_bias(t, range(TILES - 1))
-                if 1 <= t:
-                    floor_norms(t - 1)
-                add_bias(t, range(TILES - 1, TILES))
-                b, half = divmod(t, ROUNDS_PER_BATCH)
-                if b == BATCH - 1:
-                    store(b, 2, half * TILES, TILES)
-                elif half == ROUNDS_PER_BATCH - 1:
-                    store(b, 2)
-            if 1 <= t < ROUNDS:
+                add_bias(t, range(SIZES[t] - 1))
+            if 1 <= t:
+                floor_norms(t - 1)
+            if t < ROUNDS:
+                add_bias(t, range(SIZES[t] - 1, SIZES[t]))
+                store_ready(t, (2,))
+            if 1 <= t:
                 scale(t - 1)
-                b, half = divmod(t - 1, ROUNDS_PER_BATCH)
-                for w in range(2):
-                    if b == BATCH - 1:
-                        store(b, w, half * TILES, TILES)
-                    elif half == ROUNDS_PER_BATCH - 1:
-                        store(b, w)
-        finish(ROUNDS - 1)
+                store_ready(t - 1, (0, 1))

@@ -25,6 +25,7 @@ TOK_PER_PART = SEQ // P
 TILES = 4
 SIZES = (TILES,) * 15 + (2, 2)
 ROUNDS = len(SIZES)
+PAIR = 2
 X_BUFS = 8
 FIRST_SORTED = 4
 SORTED = 1
@@ -50,7 +51,8 @@ def tile_knnxlmultiheadsattention_pa_t_kernel(
         stage_pool = ctx.enter_context(tc.tile_pool(name="stage", bufs=3))
         small_pool = ctx.enter_context(tc.tile_pool(name="small", bufs=3))
         xt_pool = ctx.enter_context(tc.psum_pool(name="xt", bufs=TILES))
-        acc_pool = ctx.enter_context(tc.psum_pool(name="acc", bufs=TILES))
+        qk_pool = ctx.enter_context(tc.psum_pool(name="qk", bufs=2))
+        v_pool = ctx.enter_context(tc.psum_pool(name="v", bufs=2))
 
         starts = [divmod(sum(SIZES[:r]), TOK_PER_PART) for r in range(ROUNDS)]
         x_tiles = {}
@@ -58,7 +60,8 @@ def tile_knnxlmultiheadsattention_pa_t_kernel(
         grouped_tiles = {}
         code_tiles = {}
         plane_tiles = {}
-        acc_tiles = {}
+        qk_accs = {}
+        v_accs = {}
         stage_tiles = {}
         norm_tiles = {}
         inv_tiles = {}
@@ -116,13 +119,16 @@ def tile_knnxlmultiheadsattention_pa_t_kernel(
         def project(r):
             codes = code_tiles[r]
             planes = plane_tiles[r]
+            v_acc = v_pool.tile([P, TILES, FEAT], F32)
             for i in range(SIZES[r]):
-                acc = acc_pool.tile([P, 512], F32)
-                for cols in (slice(0, 2 * FEAT), slice(2 * FEAT, 3 * FEAT)):
-                    for g in range(PASSES):
-                        tokens = slice((i * PASSES + g) * P, (i * PASSES + g + 1) * P)
+                if i % PAIR == 0:
+                    qk_acc = qk_pool.tile([P, PAIR, 2 * FEAT], F32)
+                    qk_accs[(r, i // PAIR)] = qk_acc
+                for g in range(PASSES):
+                    tokens = slice((i * PASSES + g) * P, (i * PASSES + g + 1) * P)
+                    for acc, cols in ((qk_acc[:, i % PAIR, :], slice(0, 2 * FEAT)), (v_acc[:, i, :], slice(2 * FEAT, PROJ * FEAT))):
                         nc.tensor.matmul_mx(
-                            out=acc[:, cols],
+                            out=acc,
                             lhsT=codes[:, tokens].bitcast(FP8X4),
                             lhsT_scale=planes[:, tokens],
                             rhs=w_codes[:, g, cols].bitcast(FP8X4),
@@ -130,21 +136,30 @@ def tile_knnxlmultiheadsattention_pa_t_kernel(
                             start=(g == 0),
                             stop=(g == PASSES - 1),
                         )
-                acc_tiles[(r, i)] = acc
+            v_accs[r] = v_acc
 
-        def add_bias(r, tiles):
+        def add_bias_qk(r, pair):
             b, j = starts[r]
-            if j == 0 and b not in stage_tiles:
+            if b not in stage_tiles:
                 stage = stage_pool.tile([P, PROJ, HEADS, TOK_PER_PART, HEAD_DIM], F32)
                 stage_tiles[b] = stage
-            stage = stage_tiles[b]
-            for i in tiles:
-                nc.vector.tensor_tensor(
-                    out=stage[:, :, :, j + i, :],
-                    in0=acc_tiles[(r, i)][:, 0 : PROJ * FEAT].rearrange("p (w h d) -> p w h d", w=PROJ, h=HEADS),
-                    in1=bias_bc[:].rearrange("p (w h d) -> p w h d", w=PROJ, h=HEADS),
-                    op=ALU.add,
-                )
+            lo = j + pair * PAIR
+            nc.vector.tensor_tensor(
+                out=stage_tiles[b][:].rearrange("p w h j d -> p j (w h) d")[:, lo : lo + PAIR, 0 : 2 * HEADS, :],
+                in0=qk_accs[(r, pair)][:].rearrange("p i (c d) -> p i c d", d=HEAD_DIM),
+                in1=bias_bc[:, 0 : 2 * FEAT].rearrange("p (c d) -> p c d", d=HEAD_DIM).unsqueeze(1).to_broadcast([P, PAIR, 2 * HEADS, HEAD_DIM]),
+                op=ALU.add,
+            )
+
+        def add_bias_v(r):
+            b, j = starts[r]
+            count = SIZES[r]
+            nc.vector.tensor_tensor(
+                out=stage_tiles[b][:, 2].rearrange("p h j d -> p j h d")[:, j : j + count, :, :],
+                in0=v_accs[r][:, 0:count, :].rearrange("p i (h d) -> p i h d", d=HEAD_DIM),
+                in1=bias_bc[:, 2 * FEAT :].rearrange("p (h d) -> p h d", d=HEAD_DIM).unsqueeze(1).to_broadcast([P, count, HEADS, HEAD_DIM]),
+                op=ALU.add,
+            )
 
         def sum_squares(r):
             b, j = starts[r]
@@ -245,11 +260,12 @@ def tile_knnxlmultiheadsattention_pa_t_kernel(
             if t == 0:
                 nc.vector.tensor_copy(out=bias_bc[:], in_=spread)
             if t < ROUNDS:
-                add_bias(t, range(SIZES[t] - 1))
+                for pair in range(SIZES[t] // PAIR):
+                    add_bias_qk(t, pair)
             if 1 <= t:
                 floor_norms(t - 1)
             if t < ROUNDS:
-                add_bias(t, range(SIZES[t] - 1, SIZES[t]))
+                add_bias_v(t)
                 store_ready(t, (2,))
             if 1 <= t:
                 scale(t - 1)

@@ -22,13 +22,15 @@ PROJ = 3
 PASSES = EMB // K_PASS
 WORDS = K_PASS // 2
 TOK_PER_PART = SEQ // P
-TILES = 4
-SIZES = (TILES,) * 15 + (2, 2)
+CHUNK = 4
+RUN = 3
+SIZES = (RUN,) * 20 + (2, 2)
 ROUNDS = len(SIZES)
+ALL_TILES = sum(SIZES)
+CHUNKS = ALL_TILES // CHUNK
 PAIR = 2
 X_BUFS = 8
 FIRST_SORTED = 4
-SORTED = 1
 
 FLOPS = 2 * BATCH * SEQ * EMB * PROJ * FEAT
 
@@ -50,11 +52,11 @@ def tile_knnxlmultiheadsattention_pa_t_kernel(
         mx_pool = ctx.enter_context(tc.tile_pool(name="mx", bufs=2))
         stage_pool = ctx.enter_context(tc.tile_pool(name="stage", bufs=3))
         small_pool = ctx.enter_context(tc.tile_pool(name="small", bufs=3))
-        xt_pool = ctx.enter_context(tc.psum_pool(name="xt", bufs=TILES))
+        xt_pool = ctx.enter_context(tc.psum_pool(name="xt", bufs=4))
         qk_pool = ctx.enter_context(tc.psum_pool(name="qk", bufs=2))
         v_pool = ctx.enter_context(tc.psum_pool(name="v", bufs=2))
 
-        starts = [divmod(sum(SIZES[:r]), TOK_PER_PART) for r in range(ROUNDS)]
+        first_tile = [sum(SIZES[:r]) for r in range(ROUNDS)]
         x_tiles = {}
         sorted_tiles = {}
         grouped_tiles = {}
@@ -63,70 +65,77 @@ def tile_knnxlmultiheadsattention_pa_t_kernel(
         qk_accs = {}
         v_accs = {}
         stage_tiles = {}
+        sumsq_tiles = {}
         norm_tiles = {}
         inv_tiles = {}
 
-        def load(r, pieces=()):
-            b, j = starts[r]
-            x_sb = x_pool.tile([P, TILES, EMB], BF16)
-            for queue, lo, hi in pieces or ((nc.sync, 0, SIZES[r]),):
-                queue.dma_start(out=x_sb[:, lo:hi, :], in_=x_view[b, :, j + lo : j + hi, :])
-            x_tiles[r] = x_sb
+        def round_tiles(r):
+            return range(first_tile[r], first_tile[r] + SIZES[r])
 
-        def sort_words(r):
-            x_words = x_tiles[r][:].rearrange("p i k -> p (i k)").bitcast(F32)
-            in_order = sorted_pool.tile([P, SORTED * PASSES, 2, P], F32)
-            nc.vector.tensor_copy(
-                out=in_order[:], in_=x_words[:, 0 : SORTED * PASSES * WORDS].rearrange("p (a w u) -> p a u w", w=P, u=2)
-            )
-            sorted_tiles[r] = in_order
+        def load(c, pieces=()):
+            b, j = divmod(c * CHUNK, TOK_PER_PART)
+            x_sb = x_pool.tile([P, CHUNK, EMB], BF16)
+            for queue, lo, hi in pieces or ((nc.sync, 0, CHUNK),):
+                queue.dma_start(out=x_sb[:, lo:hi, :], in_=x_view[b, :, j + lo : j + hi, :])
+            x_tiles[c] = x_sb
+
+        def sort_words(n):
+            words = x_tiles[n // CHUNK][:, n % CHUNK, :].bitcast(F32)
+            in_order = sorted_pool.tile([P, PASSES, 2, P], F32)
+            nc.vector.tensor_copy(out=in_order[:], in_=words.rearrange("p (g w u) -> p g u w", w=P, u=2))
+            sorted_tiles[n] = in_order
 
         def transpose(r):
-            x_words = x_tiles[r][:].rearrange("p i k -> p (i k)").bitcast(F32)
-            grouped = grouped_pool.tile([P, TILES, PASSES, P, PACK], BF16, align_bytes=64)
+            grouped = grouped_pool.tile([P, RUN, PASSES, P, PACK], BF16, align_bytes=64)
             grouped_words = (
                 grouped[:]
                 .rearrange("p i g w t -> p (i g w t)")
                 .bitcast(F32)
-                .rearrange("p (i g w u) -> p i g w u", i=TILES, g=PASSES, u=2)
+                .rearrange("p (i g w u) -> p i g w u", i=RUN, g=PASSES, u=2)
             )
-            for i in range(SIZES[r]):
+            for i, n in enumerate(round_tiles(r)):
+                words = x_tiles[n // CHUNK][:, n % CHUNK, :].bitcast(F32)
                 xt = xt_pool.tile([P, PASSES, 2, P], F32)
                 for g in range(PASSES):
-                    first = (i * PASSES + g) * WORDS
                     for u in range(2):
-                        if i < SORTED and r in sorted_tiles:
-                            nc.tensor.transpose(xt[:, g, u, :], sorted_tiles[r][:, i * PASSES + g, u, :], ident[:])
+                        if n in sorted_tiles:
+                            nc.tensor.transpose(xt[:, g, u, :], sorted_tiles[n][:, g, u, :], ident[:])
                         else:
-                            nc.tensor.transpose(xt[:, g, u, :], x_words[:, first + u : first + WORDS : 2], ident[:])
+                            nc.tensor.transpose(xt[:, g, u, :], words[:, g * WORDS + u : (g + 1) * WORDS : 2], ident[:])
                 nc.scalar.copy(out=grouped_words[:, i], in_=xt[:].rearrange("p g u w -> p g w u"))
+                if n % CHUNK == CHUNK - 1 and n // CHUNK + X_BUFS < CHUNKS:
+                    load(n // CHUNK + X_BUFS)
             grouped_tiles[r] = grouped
-            if r + X_BUFS < ROUNDS:
-                load(r + X_BUFS)
 
         def quantise(r):
-            codes = mx_pool.tile([P, TILES * PASSES * P], U32, align_bytes=64)
-            planes = mx_pool.tile([P, TILES * PASSES * P], U8, align_bytes=64)
-            cols = SIZES[r] * PASSES * P
-            nc.vector.quantize_mx(
-                out=codes[:, 0:cols].bitcast(FP8X4),
-                scales=planes[:, 0:cols],
-                in_=grouped_tiles[r][:].rearrange("p i g w t -> p (i g w t)")[:, 0 : cols * PACK],
-            )
+            codes = mx_pool.tile([P, RUN * PASSES * P], U32, align_bytes=64)
+            planes = mx_pool.tile([P, RUN * PASSES * P], U8, align_bytes=64)
+            values = grouped_tiles[r][:].rearrange("p i g w t -> p (i g w t)")
+            for lo in range(0, SIZES[r], 2):
+                cols = slice(lo * PASSES * P, min(lo + 2, SIZES[r]) * PASSES * P)
+                nc.vector.quantize_mx(
+                    out=codes[:, cols].bitcast(FP8X4),
+                    scales=planes[:, cols],
+                    in_=values[:, cols.start * PACK : cols.stop * PACK],
+                )
             code_tiles[r] = codes
             plane_tiles[r] = planes
 
         def project(r):
             codes = code_tiles[r]
             planes = plane_tiles[r]
-            v_acc = v_pool.tile([P, TILES, FEAT], F32)
-            for i in range(SIZES[r]):
-                if i % PAIR == 0:
+            for i, n in enumerate(round_tiles(r)):
+                if n % CHUNK == 0:
+                    v_acc = v_pool.tile([P, CHUNK, FEAT], F32)
+                    v_accs[n // CHUNK] = v_acc
+                if n % PAIR == 0:
                     qk_acc = qk_pool.tile([P, PAIR, 2 * FEAT], F32)
-                    qk_accs[(r, i // PAIR)] = qk_acc
+                    qk_accs[n // PAIR] = qk_acc
+                qk_out = qk_accs[n // PAIR][:, n % PAIR, :]
+                v_out = v_accs[n // CHUNK][:, n % CHUNK, :]
                 for g in range(PASSES):
                     tokens = slice((i * PASSES + g) * P, (i * PASSES + g + 1) * P)
-                    for acc, cols in ((qk_acc[:, i % PAIR, :], slice(0, 2 * FEAT)), (v_acc[:, i, :], slice(2 * FEAT, PROJ * FEAT))):
+                    for acc, cols in ((qk_out, slice(0, 2 * FEAT)), (v_out, slice(2 * FEAT, PROJ * FEAT))):
                         nc.tensor.matmul_mx(
                             out=acc,
                             lhsT=codes[:, tokens].bitcast(FP8X4),
@@ -136,61 +145,59 @@ def tile_knnxlmultiheadsattention_pa_t_kernel(
                             start=(g == 0),
                             stop=(g == PASSES - 1),
                         )
-            v_accs[r] = v_acc
 
-        def add_bias_qk(r, pair):
-            b, j = starts[r]
+        def add_bias_qk(pair):
+            b, j = divmod(pair * PAIR, TOK_PER_PART)
             if b not in stage_tiles:
                 stage = stage_pool.tile([P, PROJ, HEADS, TOK_PER_PART, HEAD_DIM], F32)
                 stage_tiles[b] = stage
-            lo = j + pair * PAIR
             nc.vector.tensor_tensor(
-                out=stage_tiles[b][:].rearrange("p w h j d -> p j (w h) d")[:, lo : lo + PAIR, 0 : 2 * HEADS, :],
-                in0=qk_accs[(r, pair)][:].rearrange("p i (c d) -> p i c d", d=HEAD_DIM),
+                out=stage_tiles[b][:].rearrange("p w h j d -> p j (w h) d")[:, j : j + PAIR, 0 : 2 * HEADS, :],
+                in0=qk_accs[pair][:].rearrange("p i (c d) -> p i c d", d=HEAD_DIM),
                 in1=bias_bc[:, 0 : 2 * FEAT].rearrange("p (c d) -> p c d", d=HEAD_DIM).unsqueeze(1).to_broadcast([P, PAIR, 2 * HEADS, HEAD_DIM]),
                 op=ALU.add,
             )
 
-        def add_bias_v(r):
-            b, j = starts[r]
-            count = SIZES[r]
+        def add_bias_v(c):
+            b, j = divmod(c * CHUNK, TOK_PER_PART)
             nc.vector.tensor_tensor(
-                out=stage_tiles[b][:, 2].rearrange("p h j d -> p j h d")[:, j : j + count, :, :],
-                in0=v_accs[r][:, 0:count, :].rearrange("p i (h d) -> p i h d", d=HEAD_DIM),
-                in1=bias_bc[:, 2 * FEAT :].rearrange("p (h d) -> p h d", d=HEAD_DIM).unsqueeze(1).to_broadcast([P, count, HEADS, HEAD_DIM]),
+                out=stage_tiles[b][:, 2].rearrange("p h j d -> p j h d")[:, j : j + CHUNK, :, :],
+                in0=v_accs[c][:].rearrange("p i (h d) -> p i h d", d=HEAD_DIM),
+                in1=bias_bc[:, 2 * FEAT :].rearrange("p (h d) -> p h d", d=HEAD_DIM).unsqueeze(1).to_broadcast([P, CHUNK, HEADS, HEAD_DIM]),
                 op=ALU.add,
             )
 
-        def sum_squares(r):
-            b, j = starts[r]
-            stage = stage_tiles[b]
-            squares = small_pool.tile([P, 2, TILES, HEADS, HEAD_DIM], BF16)
-            sumsq = small_pool.tile([P, 2, TILES], F32)
-            for i in range(SIZES[r]):
+        def sum_squares(pair):
+            c = pair * PAIR // CHUNK
+            if pair * PAIR % CHUNK == 0:
+                sumsq = small_pool.tile([P, 2, CHUNK], F32)
+                sumsq_tiles[c] = sumsq
+            squares = small_pool.tile([P, 2, PAIR, HEADS, HEAD_DIM], BF16)
+            for n in range(pair * PAIR, (pair + 1) * PAIR):
+                b, j = divmod(n, TOK_PER_PART)
                 for w in range(2):
                     nc.scalar.activation(
-                        out=squares[:, w, i],
-                        in_=stage[:, w, :, j + i, :],
+                        out=squares[:, w, n % PAIR],
+                        in_=stage_tiles[b][:, w, :, j, :],
                         func=ACT.Square,
-                        accum_out=sumsq[:, w, i : i + 1],
+                        accum_out=sumsq_tiles[c][:, w, n % CHUNK : n % CHUNK + 1],
                     )
-            rnorm = small_pool.tile([P, 2, TILES], F32)
-            some = slice(0, SIZES[r])
-            nc.scalar.activation(out=rnorm[:, :, some], in_=sumsq[:, :, some], func=ACT.Abs_reciprocal_sqrt)
-            norm_tiles[r] = rnorm
+            if (pair + 1) * PAIR % CHUNK == 0:
+                rnorm = small_pool.tile([P, 2, CHUNK], F32)
+                nc.scalar.activation(out=rnorm[:], in_=sumsq_tiles[c][:], func=ACT.Abs_reciprocal_sqrt)
+                norm_tiles[c] = rnorm
 
-        def floor_norms(r):
-            inv = small_pool.tile([P, 2, TILES], F32)
-            some = slice(0, SIZES[r])
-            nc.vector.tensor_scalar_min(inv[:, :, some], norm_tiles[r][:, :, some], 1e12)
-            inv_tiles[r] = inv
+        def floor_norms(c):
+            inv = small_pool.tile([P, 2, CHUNK], F32)
+            nc.vector.tensor_scalar_min(inv[:], norm_tiles[c][:], 1e12)
+            inv_tiles[c] = inv
 
-        def scale(r):
-            b, j = starts[r]
+        def scale(c):
             for w in range(2):
-                for i in range(SIZES[r]):
-                    part = stage_tiles[b][:, w, :, j + i, :]
-                    nc.vector.tensor_scalar_mul(part, part, inv_tiles[r][:, w, i : i + 1])
+                for i in range(CHUNK):
+                    b, j = divmod(c * CHUNK + i, TOK_PER_PART)
+                    part = stage_tiles[b][:, w, :, j, :]
+                    nc.vector.tensor_scalar_mul(part, part, inv_tiles[c][:, w, i : i + 1])
 
         def store(b, w, first=0, count=TOK_PER_PART):
             run = slice(first * HEAD_DIM, (first + count) * HEAD_DIM)
@@ -199,19 +206,19 @@ def tile_knnxlmultiheadsattention_pa_t_kernel(
                 in_=stage_tiles[b][:, w].rearrange("p h j d -> p h (j d)")[:, :, run],
             )
 
-        def store_ready(r, parts):
-            b, j = starts[r]
+        def store_ready(c, parts):
+            b, j = divmod(c * CHUNK, TOK_PER_PART)
             for w in parts:
                 if b == BATCH - 1:
-                    store(b, w, j, SIZES[r])
-                elif j + SIZES[r] == TOK_PER_PART:
+                    store(b, w, j, CHUNK)
+                elif j + CHUNK == TOK_PER_PART:
                     store(b, w)
 
-        load(0, ((nc.scalar, 0, 1), (nc.scalar, 1, 2), (nc.scalar, 2, TILES)))
+        load(0, ((nc.scalar, 0, 1), (nc.scalar, 1, 2), (nc.scalar, 2, CHUNK)))
 
         ident = const.tile([P, P], F32)
         make_identity(nc, ident[:])
-        load(1, ((nc.gpsimd, 0, 2), (nc.gpsimd, 2, TILES)))
+        load(1, ((nc.gpsimd, 0, 2), (nc.gpsimd, 2, CHUNK)))
         w_codes = const.tile([P, PASSES, PROJ * FEAT], U32, align_bytes=64)
         w_planes = const.tile([P, PASSES, PROJ * FEAT], U8, align_bytes=64)
         bias_bc = const.tile([P, PROJ * FEAT], BF16)
@@ -236,9 +243,12 @@ def tile_knnxlmultiheadsattention_pa_t_kernel(
                 nc.sync.dma_start(out=w_planes[r:P:32, :, cols].bitcast(I32), in_=rows[r])
         for w, (words, scales, bias) in enumerate(weights):
             nc.sync.dma_start(out=bias_rows[0:1, w * FEAT : (w + 1) * FEAT], in_=bias.rearrange("(o n) -> o n", o=1))
-        load(2, ((nc.sync, 0, 2), (nc.sync, 2, TILES)))
+        load(2, ((nc.sync, 0, 2), (nc.sync, 2, CHUNK)))
         for r in range(3, X_BUFS):
             load(r)
+
+        def completed(r, size):
+            return [n // size for n in round_tiles(r) if n % size == size - 1] if 0 <= r < ROUNDS else []
 
         transpose(0)
         quantise(0)
@@ -251,22 +261,23 @@ def tile_knnxlmultiheadsattention_pa_t_kernel(
                 xt = xt_pool.tile([P, PASSES, 2, P], F32)
                 spread = xt[:].rearrange("p g u w -> p (g u w)")[:, 0 : PROJ * FEAT]
                 nc.tensor.matmul(out=spread, lhsT=ones[:], rhs=bias_rows[:], start=True, stop=True)
-            if 1 <= t:
-                sum_squares(t - 1)
+            for pair in completed(t - 1, PAIR):
+                sum_squares(pair)
             if t + 1 < ROUNDS:
                 quantise(t + 1)
-            if FIRST_SORTED <= t + 3 < ROUNDS and SIZES[t + 3] == TILES:
-                sort_words(t + 3)
+            if t + 3 < ROUNDS:
+                for n in round_tiles(t + 3):
+                    if n % CHUNK == 0 and n >= FIRST_SORTED * CHUNK:
+                        sort_words(n)
             if t == 0:
                 nc.vector.tensor_copy(out=bias_bc[:], in_=spread)
-            if t < ROUNDS:
-                for pair in range(SIZES[t] // PAIR):
-                    add_bias_qk(t, pair)
-            if 1 <= t:
-                floor_norms(t - 1)
-            if t < ROUNDS:
-                add_bias_v(t)
-                store_ready(t, (2,))
-            if 1 <= t:
-                scale(t - 1)
-                store_ready(t - 1, (0, 1))
+            for pair in completed(t, PAIR):
+                add_bias_qk(pair)
+            for c in completed(t - 1, CHUNK):
+                floor_norms(c)
+            for c in completed(t, CHUNK):
+                add_bias_v(c)
+                store_ready(c, (2,))
+            for c in completed(t - 1, CHUNK):
+                scale(c)
+                store_ready(c, (0, 1))

@@ -30,7 +30,7 @@ ALL_TILES = sum(SIZES)
 CHUNKS = ALL_TILES // CHUNK
 PAIR = 2
 X_BUFS = 8
-FIRST_SORTED = 4
+FIRST_SORTED = 6
 
 FLOPS = 2 * BATCH * SEQ * EMB * PROJ * FEAT
 
@@ -47,7 +47,7 @@ def tile_knnxlmultiheadsattention_pa_t_kernel(
         ctx.enter_context(tc.manual_schedule())
         const = ctx.enter_context(tc.tile_pool(name="const", bufs=1))
         x_pool = ctx.enter_context(tc.tile_pool(name="x", bufs=X_BUFS))
-        sorted_pool = ctx.enter_context(tc.tile_pool(name="sorted", bufs=3))
+        sorted_pool = ctx.enter_context(tc.tile_pool(name="sorted", bufs=4))
         grouped_pool = ctx.enter_context(tc.tile_pool(name="grouped", bufs=2))
         mx_pool = ctx.enter_context(tc.tile_pool(name="mx", bufs=2))
         stage_pool = ctx.enter_context(tc.tile_pool(name="stage", bufs=3))
@@ -82,7 +82,8 @@ def tile_knnxlmultiheadsattention_pa_t_kernel(
         def sort_words(n):
             words = x_tiles[n // CHUNK][:, n % CHUNK, :].bitcast(F32)
             in_order = sorted_pool.tile([P, PASSES, 2, P], F32)
-            nc.vector.tensor_copy(out=in_order[:], in_=words.rearrange("p (g w u) -> p g u w", w=P, u=2))
+            nc.vector.memset(in_order[:, 0, 0, 0:1], 0.0)
+            nc.gpsimd.tensor_copy(out=in_order[:], in_=words.rearrange("p (g w u) -> p g u w", w=P, u=2))
             sorted_tiles[n] = in_order
 
         def transpose(r):
@@ -266,9 +267,8 @@ def tile_knnxlmultiheadsattention_pa_t_kernel(
             if t + 1 < ROUNDS:
                 quantise(t + 1)
             if t + 3 < ROUNDS:
-                for n in round_tiles(t + 3):
-                    if n % CHUNK == 0 and n >= FIRST_SORTED * CHUNK:
-                        sort_words(n)
+                if t + 3 >= FIRST_SORTED:
+                    sort_words(first_tile[t + 3])
             if t == 0:
                 nc.vector.tensor_copy(out=bias_bc[:], in_=spread)
             for pair in completed(t, PAIR):

from contextlib import ExitStack

import concourse.mybir as mybir
from concourse.masks import make_identity

F32 = mybir.dt.float32
BF16 = mybir.dt.bfloat16
I32 = mybir.dt.int32
U32 = mybir.dt.uint32
U8 = mybir.dt.uint8
FP8X4 = mybir.dt.float8_e4m3fn_x4
ALU = mybir.AluOpType
ACT = mybir.ActivationFunctionType

P = 128
PACK = 4
K_PASS = P * PACK
BATCH, SEQ, EMB = 8, 1024, 1024
HEADS, HEAD_DIM = 2, 64
FEAT = HEADS * HEAD_DIM
PROJ = 3
PASSES = EMB // K_PASS
WORDS = K_PASS // 2
TOK_PER_PART = SEQ // P
CHUNK = 4
RUN = 3
SIZES = (RUN,) * 20 + (2, 2)
ROUNDS = len(SIZES)
ALL_TILES = sum(SIZES)
CHUNKS = ALL_TILES // CHUNK
PAIR = 2
X_BUFS = 8
FIRST_SORTED = 6

FLOPS = 2 * BATCH * SEQ * EMB * PROJ * FEAT


def tile_knnxlmultiheadsattention_pa_t_kernel(
    tc, x, wq_words, wq_scales, bq, wk_words, wk_scales, bk, wv_words, wv_scales, bv, out_q, out_k, out_v
):
    nc = tc.nc
    weights = ((wq_words, wq_scales, bq), (wk_words, wk_scales, bk), (wv_words, wv_scales, bv))
    outs = (out_q, out_k, out_v)
    x_view = x.rearrange("b (p j) k -> b p j k", j=TOK_PER_PART)

    with ExitStack() as ctx:
        ctx.enter_context(tc.manual_schedule())
        const = ctx.enter_context(tc.tile_pool(name="const", bufs=1))
        x_pool = ctx.enter_context(tc.tile_pool(name="x", bufs=X_BUFS))
        sorted_pool = ctx.enter_context(tc.tile_pool(name="sorted", bufs=4))
        grouped_pool = ctx.enter_context(tc.tile_pool(name="grouped", bufs=2))
        mx_pool = ctx.enter_context(tc.tile_pool(name="mx", bufs=2))
        stage_pool = ctx.enter_context(tc.tile_pool(name="stage", bufs=3))
        small_pool = ctx.enter_context(tc.tile_pool(name="small", bufs=3))
        xt_pool = ctx.enter_context(tc.psum_pool(name="xt", bufs=4))
        qk_pool = ctx.enter_context(tc.psum_pool(name="qk", bufs=2))
        v_pool = ctx.enter_context(tc.psum_pool(name="v", bufs=2))

        first_tile = [sum(SIZES[:r]) for r in range(ROUNDS)]
        x_tiles = {}
        sorted_tiles = {}
        grouped_tiles = {}
        code_tiles = {}
        plane_tiles = {}
        qk_accs = {}
        v_accs = {}
        stage_tiles = {}
        sumsq_tiles = {}
        norm_tiles = {}
        inv_tiles = {}

        def round_tiles(r):
            return range(first_tile[r], first_tile[r] + SIZES[r])

        def load(c, pieces=()):
            b, j = divmod(c * CHUNK, TOK_PER_PART)
            x_sb = x_pool.tile([P, CHUNK, EMB], BF16)
            for queue, lo, hi in pieces or ((nc.sync, 0, CHUNK),):
                queue.dma_start(out=x_sb[:, lo:hi, :], in_=x_view[b, :, j + lo : j + hi, :])
            x_tiles[c] = x_sb

        def sort_words(n):
            words = x_tiles[n // CHUNK][:, n % CHUNK, :].bitcast(F32)
            in_order = sorted_pool.tile([P, PASSES, 2, P], F32)
            nc.vector.memset(in_order[:, 0, 0, 0:1], 0.0)
            nc.gpsimd.tensor_copy(out=in_order[:], in_=words.rearrange("p (g w u) -> p g u w", w=P, u=2))
            sorted_tiles[n] = in_order

        def transpose(r):
            grouped = grouped_pool.tile([P, RUN, PASSES, P, PACK], BF16, align_bytes=64)
            grouped_words = (
                grouped[:]
                .rearrange("p i g w t -> p (i g w t)")
                .bitcast(F32)
                .rearrange("p (i g w u) -> p i g w u", i=RUN, g=PASSES, u=2)
            )
            for i, n in enumerate(round_tiles(r)):
                words = x_tiles[n // CHUNK][:, n % CHUNK, :].bitcast(F32)
                xt = xt_pool.tile([P, PASSES, 2, P], F32)
                for g in range(PASSES):
                    for u in range(2):
                        if n in sorted_tiles:
                            nc.tensor.transpose(xt[:, g, u, :], sorted_tiles[n][:, g, u, :], ident[:])
                        else:
                            nc.tensor.transpose(xt[:, g, u, :], words[:, g * WORDS + u : (g + 1) * WORDS : 2], ident[:])
                nc.scalar.copy(out=grouped_words[:, i], in_=xt[:].rearrange("p g u w -> p g w u"))
                if n % CHUNK == CHUNK - 1 and n // CHUNK + X_BUFS < CHUNKS:
                    load(n // CHUNK + X_BUFS)
            grouped_tiles[r] = grouped

        def quantise(r):
            codes = mx_pool.tile([P, RUN * PASSES * P], U32, align_bytes=64)
            planes = mx_pool.tile([P, RUN * PASSES * P], U8, align_bytes=64)
            values = grouped_tiles[r][:].rearrange("p i g w t -> p (i g w t)")
            for lo in range(0, SIZES[r], 2):
                cols = slice(lo * PASSES * P, min(lo + 2, SIZES[r]) * PASSES * P)
                nc.vector.quantize_mx(
                    out=codes[:, cols].bitcast(FP8X4),
                    scales=planes[:, cols],
                    in_=values[:, cols.start * PACK : cols.stop * PACK],
                )
            code_tiles[r] = codes
            plane_tiles[r] = planes

        def project(r):
            codes = code_tiles[r]
            planes = plane_tiles[r]
            for i, n in enumerate(round_tiles(r)):
                if n % CHUNK == 0:
                    v_acc = v_pool.tile([P, CHUNK, FEAT], F32)
                    v_accs[n // CHUNK] = v_acc
                if n % PAIR == 0:
                    qk_acc = qk_pool.tile([P, PAIR, 2 * FEAT], F32)
                    qk_accs[n // PAIR] = qk_acc
                qk_out = qk_accs[n // PAIR][:, n % PAIR, :]
                v_out = v_accs[n // CHUNK][:, n % CHUNK, :]
                for g in range(PASSES):
                    tokens = slice((i * PASSES + g) * P, (i * PASSES + g + 1) * P)
                    for acc, cols in ((qk_out, slice(0, 2 * FEAT)), (v_out, slice(2 * FEAT, PROJ * FEAT))):
                        nc.tensor.matmul_mx(
                            out=acc,
                            lhsT=codes[:, tokens].bitcast(FP8X4),
                            lhsT_scale=planes[:, tokens],
                            rhs=w_codes[:, g, cols].bitcast(FP8X4),
                            rhs_scale=w_planes[:, g, cols],
                            start=(g == 0),
                            stop=(g == PASSES - 1),
                        )

        def add_bias_qk(pair):
            b, j = divmod(pair * PAIR, TOK_PER_PART)
            if b not in stage_tiles:
                stage = stage_pool.tile([P, PROJ, HEADS, TOK_PER_PART, HEAD_DIM], F32)
                stage_tiles[b] = stage
            nc.vector.tensor_tensor(
                out=stage_tiles[b][:].rearrange("p w h j d -> p j (w h) d")[:, j : j + PAIR, 0 : 2 * HEADS, :],
                in0=qk_accs[pair][:].rearrange("p i (c d) -> p i c d", d=HEAD_DIM),
                in1=bias_bc[:, 0 : 2 * FEAT].rearrange("p (c d) -> p c d", d=HEAD_DIM).unsqueeze(1).to_broadcast([P, PAIR, 2 * HEADS, HEAD_DIM]),
                op=ALU.add,
            )

        def add_bias_v(c):
            b, j = divmod(c * CHUNK, TOK_PER_PART)
            nc.vector.tensor_tensor(
                out=stage_tiles[b][:, 2].rearrange("p h j d -> p j h d")[:, j : j + CHUNK, :, :],
                in0=v_accs[c][:].rearrange("p i (h d) -> p i h d", d=HEAD_DIM),
                in1=bias_bc[:, 2 * FEAT :].rearrange("p (h d) -> p h d", d=HEAD_DIM).unsqueeze(1).to_broadcast([P, CHUNK, HEADS, HEAD_DIM]),
                op=ALU.add,
            )

        def sum_squares(pair):
            c = pair * PAIR // CHUNK
            if pair * PAIR % CHUNK == 0:
                sumsq = small_pool.tile([P, 2, CHUNK], F32)
                sumsq_tiles[c] = sumsq
            squares = small_pool.tile([P, 2, PAIR, HEADS, HEAD_DIM], BF16)
            for n in range(pair * PAIR, (pair + 1) * PAIR):
                b, j = divmod(n, TOK_PER_PART)
                for w in range(2):
                    nc.scalar.activation(
                        out=squares[:, w, n % PAIR],
                        in_=stage_tiles[b][:, w, :, j, :],
                        func=ACT.Square,
                        accum_out=sumsq_tiles[c][:, w, n % CHUNK : n % CHUNK + 1],
                    )
            if (pair + 1) * PAIR % CHUNK == 0:
                rnorm = small_pool.tile([P, 2, CHUNK], F32)
                nc.scalar.activation(out=rnorm[:], in_=sumsq_tiles[c][:], func=ACT.Abs_reciprocal_sqrt)
                norm_tiles[c] = rnorm

        def floor_norms(c):
            inv = small_pool.tile([P, 2, CHUNK], F32)
            nc.vector.tensor_scalar_min(inv[:], norm_tiles[c][:], 1e12)
            inv_tiles[c] = inv

        def scale(c):
            for w in range(2):
                for i in range(CHUNK):
                    b, j = divmod(c * CHUNK + i, TOK_PER_PART)
                    part = stage_tiles[b][:, w, :, j, :]
                    nc.vector.tensor_scalar_mul(part, part, inv_tiles[c][:, w, i : i + 1])

        def store(b, w, first=0, count=TOK_PER_PART):
            run = slice(first * HEAD_DIM, (first + count) * HEAD_DIM)
            nc.sync.dma_start(
                out=outs[w][b].rearrange("h (p j) d -> p h (j d)", j=TOK_PER_PART)[:, :, run],
                in_=stage_tiles[b][:, w].rearrange("p h j d -> p h (j d)")[:, :, run],
            )

        def store_ready(c, parts):
            b, j = divmod(c * CHUNK, TOK_PER_PART)
            for w in parts:
                if b == BATCH - 1:
                    store(b, w, j, CHUNK)
                elif j + CHUNK == TOK_PER_PART:
                    store(b, w)

        load(0, ((nc.scalar, 0, 1), (nc.scalar, 1, 2), (nc.scalar, 2, CHUNK)))

        ident = const.tile([P, P], F32)
        make_identity(nc, ident[:])
        load(1, ((nc.gpsimd, 0, 2), (nc.gpsimd, 2, CHUNK)))
        w_codes = const.tile([P, PASSES, PROJ * FEAT], U32, align_bytes=64)
        w_planes = const.tile([P, PASSES, PROJ * FEAT], U8, align_bytes=64)
        bias_bc = const.tile([P, PROJ * FEAT], BF16)
        bias_rows = const.tile([P, PROJ * FEAT], BF16)
        ones = const.tile([P, P], BF16)
        nc.vector.memset(w_planes[:].rearrange("p g n -> p (g n)").bitcast(I32), 0)
        nc.vector.memset(bias_rows[:], 0.0)
        nc.vector.memset(ones[:], 1.0)
        warm = const.tile([P, 1], F32)
        nc.vector.memset(warm[:], 1.0)
        nc.scalar.activation(out=warm[:], in_=warm[:], func=ACT.Abs_reciprocal_sqrt)

        for w, (words, scales, bias) in enumerate(weights):
            cols = slice(w * FEAT, (w + 1) * FEAT)
            nc.sync.dma_start(
                out=w_codes[:, :, cols].bitcast(I32), in_=words.rearrange("g p n t -> p g (n t)").bitcast(I32)
            )
        for w, (words, scales, bias) in enumerate(weights):
            cols = slice(w * FEAT, (w + 1) * FEAT)
            rows = scales.bitcast(I32).rearrange("g (q r) n -> r q g n", r=4)
            for r in range(4):
                nc.sync.dma_start(out=w_planes[r:P:32, :, cols].bitcast(I32), in_=rows[r])
        for w, (words, scales, bias) in enumerate(weights):
            nc.sync.dma_start(out=bias_rows[0:1, w * FEAT : (w + 1) * FEAT], in_=bias.rearrange("(o n) -> o n", o=1))
        load(2, ((nc.sync, 0, 2), (nc.sync, 2, CHUNK)))
        for r in range(3, X_BUFS):
            load(r)

        def completed(r, size):
            return [n // size for n in round_tiles(r) if n % size == size - 1] if 0 <= r < ROUNDS else []

        transpose(0)
        quantise(0)
        for t in range(ROUNDS + 1):
            if t + 1 < ROUNDS:
                transpose(t + 1)
            if t < ROUNDS:
                project(t)
            if t == 0:
                xt = xt_pool.tile([P, PASSES, 2, P], F32)
                spread = xt[:].rearrange("p g u w -> p (g u w)")[:, 0 : PROJ * FEAT]
                nc.tensor.matmul(out=spread, lhsT=ones[:], rhs=bias_rows[:], start=True, stop=True)
            for pair in completed(t - 1, PAIR):
                sum_squares(pair)
            if t + 1 < ROUNDS:
                quantise(t + 1)
            if t + 3 < ROUNDS:
                if t + 3 >= FIRST_SORTED:
                    sort_words(first_tile[t + 3])
            if t == 0:
                nc.vector.tensor_copy(out=bias_bc[:], in_=spread)
            for pair in completed(t, PAIR):
                add_bias_qk(pair)
            for c in completed(t - 1, CHUNK):
                floor_norms(c)
            for c in completed(t, CHUNK):
                add_bias_v(c)
                store_ready(c, (2,))
            for c in completed(t - 1, CHUNK):
                scale(c)
                store_ready(c, (0, 1))
